import numpy as np
import ml_dtypes


def mxq(x, axis, fmt="e4m3"):
    dtype, down = {"e4m3": (ml_dtypes.float8_e4m3fn, 7), "e5m2": (ml_dtypes.float8_e5m2, 14)}[fmt]
    v = np.moveaxis(np.asarray(x, np.float32).astype(ml_dtypes.bfloat16).astype(np.float64), axis, -1)
    blocks = v.reshape(v.shape[:-1] + (-1, 32))
    amax = np.abs(blocks).max(-1, keepdims=True)
    byte = np.maximum(np.where(amax > 0, np.frexp(amax)[1] - 1 + 127, 0) - down, 1)
    scale = np.exp2(byte - 127.0)
    codes = (blocks / scale).astype(np.float32).astype(dtype).astype(np.float64)
    return np.moveaxis((codes * scale).reshape(v.shape), -1, axis)


WIDE = False


def mx_kscale(k):
    if not WIDE:
        return np.ones(k)
    levels = np.array([10, -10, 5, -5, 0])
    a = np.random.permutation(np.resize(levels, k // 512 * 4)).reshape(k // 512, 4)
    idx = np.arange(k)
    return np.exp2(a[idx // 512, idx % 128 // 32])


BF16 = ml_dtypes.bfloat16


def bf(x):
    return np.asarray(x, np.float32).astype(BF16)


def f64(x):
    return np.asarray(x).astype(np.float64)


B, S, D, H, DC, DR = 4, 128, 2048, 16, 512, 64
HALF = DR // 2
ROPE_BASE = 10000.0


def rope_tables():
    inv_freq = 1.0 / ROPE_BASE ** (np.arange(0, DR, 2) / DR)
    ang = np.arange(S)[:, None] * inv_freq[None, :]
    return np.cos(ang), np.sin(ang)


def setup_inputs():
    s = mx_kscale(D)
    t = np.array(mx_kscale(DC), dtype=np.float64)
    t[HALF:DR] = t[:HALF]
    return {"x": bf(np.random.standard_normal((B, S, D)) * s),
            "W_c": bf(np.random.standard_normal((D, DC)) / np.sqrt(D) / s[:, None] * t),
            "b_c": bf(np.random.standard_normal(DC) * 0.3 * t),
            "W_d": bf(np.random.standard_normal((DC, 3 * D)) / np.sqrt(DC) / t[:, None]),
            "b_d": bf(np.random.standard_normal(3 * D) * 0.3)}


def reference(x, W_c, b_c, W_d, b_d):
    cos, sin = rope_tables()
    c = (mxq(f64(x), 2, "e4m3") @ mxq(f64(W_c), 0, "e4m3")) + f64(b_c)
    c1, c2 = c[..., :HALF], c[..., HALF:DR]
    c = np.concatenate([c1 * cos - c2 * sin, c1 * sin + c2 * cos, c[..., DR:]], axis=-1)
    return (mxq(c, 2, "e4m3") @ mxq(f64(W_d), 0, "e4m3")) + f64(b_d)

@@ -1,0 +1,246 @@
+import math
+
+import concourse.mybir as mybir
+from concourse.masks import make_identity
+
+F32 = mybir.dt.float32
+BF16 = mybir.dt.bfloat16
+I32 = mybir.dt.int32
+U32 = mybir.dt.uint32
+U8 = mybir.dt.uint8
+FP8X4 = mybir.dt.float8_e4m3fn_x4
+ALU = mybir.AluOpType
+ACT = mybir.ActivationFunctionType
+
+P = 128
+PACK = 4
+K_PASS = P * PACK
+N_TILE = 512
+
+B, S, D, DC, DR = 4, 128, 2048, 512, 64
+D_OUT = 3 * D
+HALF = DR // 2
+ROPE_BASE = 10000.0
+D_PASSES = D // K_PASS
+LATENT_ROWS = DC // PACK
+ROT_ROWS = DR // PACK
+HALF_ROWS = HALF // PACK
+
+W_D_LOAD_COLS = 1024
+STORE_COLS = 1024
+ROUND_MAGIC = 1.5 * 2.0**23
+
+FLOPS = 2 * B * S * D * DC + 2 * B * S * DC * D_OUT
+
+
+def regroup_rows(copy, grouped, rows):
+    copy(
+        out=grouped.rearrange("p (c i) j -> p c j i", i=4),
+        in_=rows.rearrange("p j (c i) -> p c j i", i=4),
+    )
+
+
+def tile_deepseekmla_pa_kernel(tc, x, W_c, b_c, W_d, b_d, out):
+    nc = tc.nc
+    with (
+        tc.tile_pool(name="consts", bufs=1) as consts,
+        tc.tile_pool(name="keep", bufs=1) as keep,
+        tc.tile_pool(name="x_stage", bufs=2) as x_stage,
+        tc.tile_pool(name="w_stage", bufs=4) as w_stage,
+        tc.tile_pool(name="rot_stage", bufs=2) as rot_stage,
+        tc.tile_pool(name="out_stage", bufs=2 * B) as out_stage,
+        tc.psum_pool(name="psum_t", bufs=2) as psum_t,
+        tc.psum_pool(name="psum_c", bufs=2) as psum_c,
+        tc.psum_pool(name="psum_o", bufs=4) as psum_o,
+    ):
+        wc_raw = keep.tile([P, D_PASSES, PACK, DC], BF16)
+        wc_rows = W_c.rearrange("(g p j) c -> g p j c", p=P, j=PACK)
+        for g in range(D_PASSES):
+            nc.sync.dma_start(out=wc_raw[:, g], in_=wc_rows[g])
+        x_sb = keep.tile([P, B, D], BF16)
+        for b in range(B):
+            nc.sync.dma_start(out=x_sb[:, b, :], in_=x[b])
+        bc_all = consts.tile([P, DC], BF16)
+        nc.sync.dma_start(out=bc_all[:], in_=b_c.partition_broadcast(P))
+        wd_raw = keep.tile([P, PACK, D_OUT], BF16)
+        wd_rows = W_d.rearrange("(p j) n -> p j n", j=PACK)
+        bd_all = consts.tile([P, D_OUT], BF16)
+        for first in range(0, D_OUT, W_D_LOAD_COLS):
+            cols = slice(first, first + W_D_LOAD_COLS)
+            nc.sync.dma_start(out=wd_raw[:, :, cols], in_=wd_rows[:, :, cols])
+            if first == 0:
+                nc.sync.dma_start(out=bd_all[:], in_=b_d.partition_broadcast(P))
+
+        ident = consts.tile([P, P], F32)
+        make_identity(nc, ident[:])
+
+        position_i = consts.tile([P, 1], I32)
+        nc.gpsimd.iota(position_i[:], pattern=[[0, 1]], base=0, channel_multiplier=1)
+        position = consts.tile([P, 1], F32)
+        nc.vector.tensor_copy(out=position[:], in_=position_i[:])
+        turns = consts.tile([P, 2, PACK, HALF_ROWS], F32)
+        for j in range(HALF):
+            turns_per_position = 1.0 / ROPE_BASE ** (2 * j / DR) / (2.0 * math.pi)
+            nc.vector.tensor_scalar_mul(
+                out=turns[:, 0, j % PACK, j // PACK : j // PACK + 1],
+                in0=position[:],
+                scalar1=turns_per_position,
+            )
+        nc.vector.tensor_scalar_add(out=turns[:, 1], in0=turns[:, 0], scalar1=0.25)
+        whole_turns = consts.tile([P, 2, PACK, HALF_ROWS], F32)
+        nc.vector.tensor_scalar_add(out=whole_turns[:], in0=turns[:], scalar1=ROUND_MAGIC)
+        minus_part_turn = consts.tile([P, 2, PACK, HALF_ROWS], F32)
+        nc.vector.scalar_tensor_tensor(
+            out=minus_part_turn[:].rearrange("p s t m -> p (s t m)"),
+            in0=whole_turns[:].rearrange("p s t m -> p (s t m)"),
+            scalar=ROUND_MAGIC,
+            in1=turns[:].rearrange("p s t m -> p (s t m)"),
+            op0=ALU.subtract,
+            op1=ALU.subtract,
+        )
+        sin_cos = consts.tile([P, 2, PACK, 2, HALF_ROWS], F32)
+        for h in range(2):
+            nc.scalar.activation(
+                out=sin_cos[:, :, :, h, :],
+                in_=minus_part_turn[:],
+                func=ACT.Sin,
+                scale=-2.0 * math.pi,
+            )
+        sin_a = sin_cos[:, 0].rearrange("p t h m -> p t (h m)")
+        cos_a = sin_cos[:, 1].rearrange("p t h m -> p t (h m)")
+
+        wc_codes = keep.tile([P, D_PASSES, DC], U32, align_bytes=64)
+        wc_scales = keep.tile([P, D_PASSES, DC], U8, align_bytes=64)
+        for g in range(D_PASSES):
+            wc_grouped = w_stage.tile([P, DC, PACK], BF16, align_bytes=64, tag="w_grouped")
+            copy = nc.vector.tensor_copy if g % 2 == 0 else nc.scalar.copy
+            regroup_rows(copy, wc_grouped[:], wc_raw[:, g])
+            nc.vector.quantize_mx(
+                out=wc_codes[:, g, :].bitcast(FP8X4),
+                scales=wc_scales[:, g, :],
+                in_=wc_grouped[:].rearrange("p c j -> p (c j)"),
+            )
+
+        x_codes = keep.tile([P, B, D_PASSES, S], U32, align_bytes=64)
+        x_scales = keep.tile([P, B, D_PASSES, S], U8, align_bytes=64)
+        c_f32 = keep.tile([P, B, PACK, LATENT_ROWS], F32)
+        r_grouped = keep.tile([P, B, S * PACK], BF16, align_bytes=64)
+        r_codes = keep.tile([P, B, S], U32, align_bytes=64)
+        r_scales = keep.tile([P, B, S], U8, align_bytes=64)
+        for b in range(B):
+            x_words = x_sb[:, b, :].bitcast(F32)
+            x_grouped = x_stage.tile([P, D_PASSES * S * PACK], BF16, align_bytes=64)
+            x_grouped_words = x_grouped[:].bitcast(F32).rearrange(
+                "p (g r u) -> p g r u", g=D_PASSES, u=2
+            )
+            for g_pair in range(0, D_PASSES, 2):
+                x_t = psum_t.tile([P, 2, 2, S], F32, tag="transposed")
+                for g in range(2):
+                    first_word = (g_pair + g) * (K_PASS // 2)
+                    for u in range(2):
+                        nc.tensor.transpose(
+                            out=x_t[:, g, u, :],
+                            in_=x_words[:, first_word + u : first_word + K_PASS // 2 : 2],
+                            identity=ident[:],
+                        )
+                nc.scalar.copy(
+                    out=x_grouped_words[:, g_pair : g_pair + 2],
+                    in_=x_t[:].rearrange("p g u r -> p g r u"),
+                )
+            nc.vector.quantize_mx(
+                out=x_codes[:, b].rearrange("p g r -> p (g r)").bitcast(FP8X4),
+                scales=x_scales[:, b].rearrange("p g r -> p (g r)"),
+                in_=x_grouped[:],
+            )
+
+            c_ps = psum_c.tile([P, DC], F32)
+            for g in range(D_PASSES):
+                nc.tensor.matmul_mx(
+                    out=c_ps[:],
+                    lhsT=x_codes[:, b, g, :].bitcast(FP8X4),
+                    lhsT_scale=x_scales[:, b, g, :],
+                    rhs=wc_codes[:, g, :].bitcast(FP8X4),
+                    rhs_scale=wc_scales[:, g, :],
+                    start=(g == 0),
+                    stop=(g == D_PASSES - 1),
+                )
+            nc.vector.tensor_tensor(
+                out=c_f32[:, b],
+                in0=c_ps[:].rearrange("p (m t) -> p t m", t=PACK),
+                in1=bc_all[:].rearrange("p (m t) -> p t m", t=PACK),
+                op=ALU.add,
+            )
+
+            first_half = slice(0, HALF_ROWS)
+            second_half = slice(HALF_ROWS, ROT_ROWS)
+            times_cos = rot_stage.tile([P, PACK, ROT_ROWS], F32)
+            times_sin = rot_stage.tile([P, PACK, ROT_ROWS], F32)
+            nc.vector.tensor_tensor(
+                out=times_cos[:], in0=c_f32[:, b, :, 0:ROT_ROWS], in1=cos_a, op=ALU.mult
+            )
+            nc.vector.tensor_tensor(
+                out=times_sin[:], in0=c_f32[:, b, :, 0:ROT_ROWS], in1=sin_a, op=ALU.mult
+            )
+            nc.vector.tensor_tensor(
+                out=c_f32[:, b, :, first_half],
+                in0=times_cos[:, :, first_half],
+                in1=times_sin[:, :, second_half],
+                op=ALU.subtract,
+            )
+            nc.vector.tensor_tensor(
+                out=c_f32[:, b, :, second_half],
+                in0=times_cos[:, :, second_half],
+                in1=times_sin[:, :, first_half],
+                op=ALU.add,
+            )
+
+            r_t = psum_t.tile([P, PACK, S], F32, tag="transposed")
+            for t in range(PACK):
+                nc.tensor.transpose(out=r_t[:, t, :], in_=c_f32[:, b, t, :], identity=ident[:])
+            nc.scalar.copy(
+                out=r_grouped[:, b, :].rearrange("p (r t) -> p r t", t=PACK),
+                in_=r_t[:].rearrange("p t r -> p r t"),
+            )
+            nc.vector.quantize_mx(
+                out=r_codes[:, b, :].bitcast(FP8X4),
+                scales=r_scales[:, b, :],
+                in_=r_grouped[:, b, :],
+            )
+
+        wd_codes = keep.tile([P, D_OUT], U32, align_bytes=64)
+        wd_scales = keep.tile([P, D_OUT], U8, align_bytes=64)
+        for store_first in range(0, D_OUT, STORE_COLS):
+            out_sb = [
+                out_stage.tile([P, STORE_COLS], F32, tag="out_sb", name="out_sb_%d" % b)
+                for b in range(B)
+            ]
+            for first in range(store_first, store_first + STORE_COLS, N_TILE):
+                cols = slice(first, first + N_TILE)
+                wd_grouped = w_stage.tile([P, N_TILE, PACK], BF16, align_bytes=64, tag="w_grouped")
+                regroup_rows(nc.scalar.copy, wd_grouped[:], wd_raw[:, :, cols])
+                nc.vector.quantize_mx(
+                    out=wd_codes[:, cols].bitcast(FP8X4),
+                    scales=wd_scales[:, cols],
+                    in_=wd_grouped[:].rearrange("p c j -> p (c j)"),
+                )
+                for b in range(B):
+                    o_ps = psum_o.tile([P, N_TILE], F32)
+                    nc.tensor.matmul_mx(
+                        out=o_ps[:],
+                        lhsT=r_codes[:, b, :].bitcast(FP8X4),
+                        lhsT_scale=r_scales[:, b, :],
+                        rhs=wd_codes[:, cols].bitcast(FP8X4),
+                        rhs_scale=wd_scales[:, cols],
+                        start=True,
+                        stop=True,
+                    )
+                    nc.vector.tensor_tensor(
+                        out=out_sb[b][:, first - store_first : first - store_first + N_TILE],
+                        in0=o_ps[:],
+                        in1=bd_all[:, cols],
+                        op=ALU.add,
+                    )
+            for b in range(B):
+                nc.sync.dma_start(
+                    out=out[b, :, store_first : store_first + STORE_COLS], in_=out_sb[b][:]
+                )

@@ -28,6 +28,12 @@ HALF_ROWS = HALF // PACK
 
 W_D_LOAD_COLS = 1024
 STORE_COLS = 1024
+CHUNKS = D_OUT // N_TILE
+CHUNKS_PER_STORE = STORE_COLS // N_TILE
+PSUM_BANKS = 8
+C_LAG = 2
+R_LAG = 3
+REGROUP_AHEAD = 2
 ROUND_MAGIC = 1.5 * 2.0**23
 
 FLOPS = 2 * B * S * D * DC + 2 * B * S * DC * D_OUT
@@ -49,9 +55,8 @@ def tile_deepseekmla_pa_kernel(tc, x, W_c, b_c, W_d, b_d, out):
         tc.tile_pool(name="w_stage", bufs=4) as w_stage,
         tc.tile_pool(name="rot_stage", bufs=2) as rot_stage,
         tc.tile_pool(name="out_stage", bufs=2 * B) as out_stage,
-        tc.psum_pool(name="psum_t", bufs=2) as psum_t,
-        tc.psum_pool(name="psum_c", bufs=2) as psum_c,
-        tc.psum_pool(name="psum_o", bufs=4) as psum_o,
+        tc.psum_pool(name="psum", bufs=PSUM_BANKS) as psum,
+        tc.manual_schedule(),
     ):
         wc_raw = keep.tile([P, D_PASSES, PACK, DC], BF16)
         wc_rows = W_c.rearrange("(g p j) c -> g p j c", p=P, j=PACK)
@@ -62,13 +67,15 @@ def tile_deepseekmla_pa_kernel(tc, x, W_c, b_c, W_d, b_d, out):
             nc.sync.dma_start(out=x_sb[:, b, :], in_=x[b])
         bc_all = consts.tile([P, DC], BF16)
         nc.sync.dma_start(out=bc_all[:], in_=b_c.partition_broadcast(P))
-        wd_raw = keep.tile([P, PACK, D_OUT], BF16)
         wd_rows = W_d.rearrange("(p j) n -> p j n", j=PACK)
+        wd_raw = []
         bd_all = consts.tile([P, D_OUT], BF16)
-        for first in range(0, D_OUT, W_D_LOAD_COLS):
-            cols = slice(first, first + W_D_LOAD_COLS)
-            nc.sync.dma_start(out=wd_raw[:, :, cols], in_=wd_rows[:, :, cols])
-            if first == 0:
+        for i in range(D_OUT // W_D_LOAD_COLS):
+            wd_raw.append(keep.tile([P, PACK, W_D_LOAD_COLS], BF16, name="wd_raw_%d" % i))
+            nc.sync.dma_start(
+                out=wd_raw[i][:], in_=wd_rows[:, :, i * W_D_LOAD_COLS : (i + 1) * W_D_LOAD_COLS]
+            )
+            if i == 0:
                 nc.sync.dma_start(out=bd_all[:], in_=b_d.partition_broadcast(P))
 
         ident = consts.tile([P, P], F32)
@@ -111,15 +118,24 @@ def tile_deepseekmla_pa_kernel(tc, x, W_c, b_c, W_d, b_d, out):
 
         wc_codes = keep.tile([P, D_PASSES, DC], U32, align_bytes=64)
         wc_scales = keep.tile([P, D_PASSES, DC], U8, align_bytes=64)
-        for g in range(D_PASSES):
-            wc_grouped = w_stage.tile([P, DC, PACK], BF16, align_bytes=64, tag="w_grouped")
-            copy = nc.vector.tensor_copy if g % 2 == 0 else nc.scalar.copy
-            regroup_rows(copy, wc_grouped[:], wc_raw[:, g])
+        wc_grouped = [
+            w_stage.tile([P, DC, PACK], BF16, align_bytes=64, tag="w_grouped", name="wc_grouped_%d" % g)
+            for g in range(D_PASSES)
+        ]
+
+        def quantise_wc(g):
             nc.vector.quantize_mx(
                 out=wc_codes[:, g, :].bitcast(FP8X4),
                 scales=wc_scales[:, g, :],
-                in_=wc_grouped[:].rearrange("p c j -> p (c j)"),
+                in_=wc_grouped[g][:].rearrange("p c j -> p (c j)"),
             )
+
+        for g in range(D_PASSES):
+            copy = nc.vector.tensor_copy if g % 2 == 0 else nc.scalar.copy
+            regroup_rows(copy, wc_grouped[g][:], wc_raw[:, g])
+            if g > 0:
+                quantise_wc(g - 1)
+        quantise_wc(D_PASSES - 1)
 
         x_codes = keep.tile([P, B, D_PASSES, S], U32, align_bytes=64)
         x_scales = keep.tile([P, B, D_PASSES, S], U8, align_bytes=64)
@@ -127,14 +143,15 @@ def tile_deepseekmla_pa_kernel(tc, x, W_c, b_c, W_d, b_d, out):
         r_grouped = keep.tile([P, B, S * PACK], BF16, align_bytes=64)
         r_codes = keep.tile([P, B, S], U32, align_bytes=64)
         r_scales = keep.tile([P, B, S], U8, align_bytes=64)
-        for b in range(B):
+
+        def quantise_x(b):
             x_words = x_sb[:, b, :].bitcast(F32)
             x_grouped = x_stage.tile([P, D_PASSES * S * PACK], BF16, align_bytes=64)
             x_grouped_words = x_grouped[:].bitcast(F32).rearrange(
                 "p (g r u) -> p g r u", g=D_PASSES, u=2
             )
             for g_pair in range(0, D_PASSES, 2):
-                x_t = psum_t.tile([P, 2, 2, S], F32, tag="transposed")
+                x_t = psum.tile([P, 2, 2, S], F32, tag="bank")
                 for g in range(2):
                     first_word = (g_pair + g) * (K_PASS // 2)
                     for u in range(2):
@@ -153,7 +170,8 @@ def tile_deepseekmla_pa_kernel(tc, x, W_c, b_c, W_d, b_d, out):
                 in_=x_grouped[:],
             )
 
-            c_ps = psum_c.tile([P, DC], F32)
+        def compress_and_rotate(b):
+            c_ps = psum.tile([P, DC], F32, tag="bank")
             for g in range(D_PASSES):
                 nc.tensor.matmul_mx(
                     out=c_ps[:],
@@ -170,7 +188,6 @@ def tile_deepseekmla_pa_kernel(tc, x, W_c, b_c, W_d, b_d, out):
                 in1=bc_all[:].rearrange("p (m t) -> p t m", t=PACK),
                 op=ALU.add,
             )
-
             first_half = slice(0, HALF_ROWS)
             second_half = slice(HALF_ROWS, ROT_ROWS)
             times_cos = rot_stage.tile([P, PACK, ROT_ROWS], F32)
@@ -194,7 +211,8 @@ def tile_deepseekmla_pa_kernel(tc, x, W_c, b_c, W_d, b_d, out):
                 op=ALU.add,
             )
 
-            r_t = psum_t.tile([P, PACK, S], F32, tag="transposed")
+        def quantise_r(b):
+            r_t = psum.tile([P, PACK, S], F32, tag="bank")
             for t in range(PACK):
                 nc.tensor.transpose(out=r_t[:, t, :], in_=c_f32[:, b, t, :], identity=ident[:])
             nc.scalar.copy(
@@ -209,38 +227,65 @@ def tile_deepseekmla_pa_kernel(tc, x, W_c, b_c, W_d, b_d, out):
 
         wd_codes = keep.tile([P, D_OUT], U32, align_bytes=64)
         wd_scales = keep.tile([P, D_OUT], U8, align_bytes=64)
-        for store_first in range(0, D_OUT, STORE_COLS):
-            out_sb = [
-                out_stage.tile([P, STORE_COLS], F32, tag="out_sb", name="out_sb_%d" % b)
-                for b in range(B)
-            ]
-            for first in range(store_first, store_first + STORE_COLS, N_TILE):
-                cols = slice(first, first + N_TILE)
-                wd_grouped = w_stage.tile([P, N_TILE, PACK], BF16, align_bytes=64, tag="w_grouped")
-                regroup_rows(nc.scalar.copy, wd_grouped[:], wd_raw[:, :, cols])
-                nc.vector.quantize_mx(
-                    out=wd_codes[:, cols].bitcast(FP8X4),
-                    scales=wd_scales[:, cols],
-                    in_=wd_grouped[:].rearrange("p c j -> p (c j)"),
-                )
-                for b in range(B):
-                    o_ps = psum_o.tile([P, N_TILE], F32)
-                    nc.tensor.matmul_mx(
-                        out=o_ps[:],
-                        lhsT=r_codes[:, b, :].bitcast(FP8X4),
-                        lhsT_scale=r_scales[:, b, :],
-                        rhs=wd_codes[:, cols].bitcast(FP8X4),
-                        rhs_scale=wd_scales[:, cols],
-                        start=True,
-                        stop=True,
-                    )
-                    nc.vector.tensor_tensor(
-                        out=out_sb[b][:, first - store_first : first - store_first + N_TILE],
-                        in0=o_ps[:],
-                        in1=bd_all[:, cols],
-                        op=ALU.add,
-                    )
+        wd_grouped = {}
+
+        def regroup_wd(n):
+            wd_grouped[n] = w_stage.tile(
+                [P, N_TILE, PACK], BF16, align_bytes=64, tag="w_grouped", name="wd_grouped_%d" % n
+            )
+            load, place = divmod(n * N_TILE, W_D_LOAD_COLS)
+            regroup_rows(nc.scalar.copy, wd_grouped[n][:], wd_raw[load][:, :, place : place + N_TILE])
+
+        def quantise_wd(n):
+            cols = slice(n * N_TILE, (n + 1) * N_TILE)
+            nc.vector.quantize_mx(
+                out=wd_codes[:, cols].bitcast(FP8X4),
+                scales=wd_scales[:, cols],
+                in_=wd_grouped[n][:].rearrange("p c j -> p (c j)"),
+            )
+
+        for step in range(B + R_LAG):
+            if step < B:
+                quantise_x(step)
+            if C_LAG <= step < B + C_LAG:
+                compress_and_rotate(step - C_LAG)
+            if step >= R_LAG:
+                quantise_r(step - R_LAG)
+            if step >= B + R_LAG - REGROUP_AHEAD:
+                regroup_wd(step - (B + R_LAG - REGROUP_AHEAD))
+        quantise_wd(0)
+
+        out_sb = {}
+        for n in range(CHUNKS):
+            if n + REGROUP_AHEAD < CHUNKS:
+                regroup_wd(n + REGROUP_AHEAD)
+            cols = slice(n * N_TILE, (n + 1) * N_TILE)
+            place = (n % CHUNKS_PER_STORE) * N_TILE
+            o_ps = {}
             for b in range(B):
-                nc.sync.dma_start(
-                    out=out[b, :, store_first : store_first + STORE_COLS], in_=out_sb[b][:]
+                if place == 0:
+                    out_sb[b] = out_stage.tile([P, STORE_COLS], F32, tag="out_sb", name="out_sb_%d" % b)
+                o_ps[b] = psum.tile([P, N_TILE], F32, tag="bank", name="o_ps_%d" % b)
+                nc.tensor.matmul_mx(
+                    out=o_ps[b][:],
+                    lhsT=r_codes[:, b, :].bitcast(FP8X4),
+                    lhsT_scale=r_scales[:, b, :],
+                    rhs=wd_codes[:, cols].bitcast(FP8X4),
+                    rhs_scale=wd_scales[:, cols],
+                    start=True,
+                    stop=True,
                 )
+            for b in range(B):
+                if b == B // 2 and n + 1 < CHUNKS:
+                    quantise_wd(n + 1)
+                nc.vector.tensor_tensor(
+                    out=out_sb[b][:, place : place + N_TILE],
+                    in0=o_ps[b][:],
+                    in1=bd_all[:, cols],
+                    op=ALU.add,
+                )
+                if place + N_TILE == STORE_COLS:
+                    store_first = (n + 1) * N_TILE - STORE_COLS
+                    nc.sync.dma_start(
+                        out=out[b, :, store_first : store_first + STORE_COLS], in_=out_sb[b][:]
+                    )

@@ -27,13 +27,16 @@ ROT_ROWS = DR // PACK
 HALF_ROWS = HALF // PACK
 
 W_D_LOAD_COLS = 1024
-STORE_COLS = 1024
+STORE_COLS = 512
+REGROUP_COLS = 256
 CHUNKS = D_OUT // N_TILE
 CHUNKS_PER_STORE = STORE_COLS // N_TILE
 PSUM_BANKS = 8
 C_LAG = 2
 R_LAG = 3
 REGROUP_AHEAD = 2
+PIECES = N_TILE // REGROUP_COLS
+assert B == REGROUP_AHEAD * PIECES
 ROUND_MAGIC = 1.5 * 2.0**23
 
 FLOPS = 2 * B * S * D * DC + 2 * B * S * DC * D_OUT
@@ -131,8 +134,7 @@ def tile_deepseekmla_pa_kernel(tc, x, W_c, b_c, W_d, b_d, out):
             )
 
         for g in range(D_PASSES):
-            copy = nc.vector.tensor_copy if g % 2 == 0 else nc.scalar.copy
-            regroup_rows(copy, wc_grouped[g][:], wc_raw[:, g])
+            regroup_rows(nc.vector.tensor_copy, wc_grouped[g][:], wc_raw[:, g])
             if g > 0:
                 quantise_wc(g - 1)
         quantise_wc(D_PASSES - 1)
@@ -229,12 +231,18 @@ def tile_deepseekmla_pa_kernel(tc, x, W_c, b_c, W_d, b_d, out):
         wd_scales = keep.tile([P, D_OUT], U8, align_bytes=64)
         wd_grouped = {}
 
-        def regroup_wd(n):
-            wd_grouped[n] = w_stage.tile(
-                [P, N_TILE, PACK], BF16, align_bytes=64, tag="w_grouped", name="wd_grouped_%d" % n
+        def regroup_wd(n, piece):
+            if piece == 0:
+                wd_grouped[n] = w_stage.tile(
+                    [P, N_TILE, PACK], BF16, align_bytes=64, tag="w_grouped", name="wd_grouped_%d" % n
+                )
+            to = piece * REGROUP_COLS
+            load, place = divmod(n * N_TILE + to, W_D_LOAD_COLS)
+            regroup_rows(
+                nc.scalar.copy,
+                wd_grouped[n][:, to : to + REGROUP_COLS, :],
+                wd_raw[load][:, :, place : place + REGROUP_COLS],
             )
-            load, place = divmod(n * N_TILE, W_D_LOAD_COLS)
-            regroup_rows(nc.scalar.copy, wd_grouped[n][:], wd_raw[load][:, :, place : place + N_TILE])
 
         def quantise_wd(n):
             cols = slice(n * N_TILE, (n + 1) * N_TILE)
@@ -251,14 +259,16 @@ def tile_deepseekmla_pa_kernel(tc, x, W_c, b_c, W_d, b_d, out):
                 compress_and_rotate(step - C_LAG)
             if step >= R_LAG:
                 quantise_r(step - R_LAG)
-            if step >= B + R_LAG - REGROUP_AHEAD:
-                regroup_wd(step - (B + R_LAG - REGROUP_AHEAD))
-        quantise_wd(0)
+                n, piece = divmod(step - R_LAG, PIECES)
+                regroup_wd(n, piece)
+                if (n, piece) == (1, 0):
+                    quantise_wd(0)
 
         out_sb = {}
         for n in range(CHUNKS):
             if n + REGROUP_AHEAD < CHUNKS:
-                regroup_wd(n + REGROUP_AHEAD)
+                for piece in range(PIECES):
+                    regroup_wd(n + REGROUP_AHEAD, piece)
             cols = slice(n * N_TILE, (n + 1) * N_TILE)
             place = (n % CHUNKS_PER_STORE) * N_TILE
             o_ps = {}

@@ -29,6 +29,7 @@ HALF_ROWS = HALF // PACK
 W_D_LOAD_COLS = 1024
 STORE_COLS = 512
 REGROUP_COLS = 256
+BIAS_COLS = 1024
 CHUNKS = D_OUT // N_TILE
 CHUNKS_PER_STORE = STORE_COLS // N_TILE
 PSUM_BANKS = 8
@@ -68,24 +69,40 @@ def tile_deepseekmla_pa_kernel(tc, x, W_c, b_c, W_d, b_d, out):
         x_sb = keep.tile([P, B, D], BF16)
         for b in range(B):
             nc.sync.dma_start(out=x_sb[:, b, :], in_=x[b])
-        bc_all = consts.tile([P, DC], BF16)
-        nc.sync.dma_start(out=bc_all[:], in_=b_c.partition_broadcast(P))
         wd_rows = W_d.rearrange("(p j) n -> p j n", j=PACK)
         wd_raw = []
-        bd_all = consts.tile([P, D_OUT], BF16)
         for i in range(D_OUT // W_D_LOAD_COLS):
             wd_raw.append(keep.tile([P, PACK, W_D_LOAD_COLS], BF16, name="wd_raw_%d" % i))
             nc.sync.dma_start(
                 out=wd_raw[i][:], in_=wd_rows[:, :, i * W_D_LOAD_COLS : (i + 1) * W_D_LOAD_COLS]
             )
-            if i == 0:
-                nc.sync.dma_start(out=bd_all[:], in_=b_d.partition_broadcast(P))
-
-        ident = consts.tile([P, P], F32)
-        make_identity(nc, ident[:])
 
         position_i = consts.tile([P, 1], I32)
         nc.gpsimd.iota(position_i[:], pattern=[[0, 1]], base=0, channel_multiplier=1)
+        bias_rows = consts.tile([P, D_OUT + DC], BF16)
+        nc.gpsimd.memset(bias_rows[:].bitcast(F32), 0.0)
+        nc.scalar.dma_start(out=bias_rows[0:1, 0:D_OUT], in_=b_d.rearrange("(o n) -> o n", o=1))
+        nc.scalar.dma_start(out=bias_rows[0:1, D_OUT:], in_=b_c.rearrange("(o n) -> o n", o=1))
+        ones = consts.tile([P, P], BF16)
+        nc.gpsimd.memset(ones[:], 1.0)
+        ident = consts.tile([P, P], F32)
+        make_identity(nc, ident[:])
+        bias_all = consts.tile([P, D_OUT + DC], BF16)
+        bd_all = bias_all[:, 0:D_OUT]
+        bc_all = bias_all[:, D_OUT:]
+
+        def broadcast_bias(first, cols):
+            spread = psum.tile([P, cols], BF16, tag="bank")
+            for at in range(0, cols, N_TILE):
+                nc.tensor.matmul(
+                    out=spread[:, at : at + N_TILE],
+                    lhsT=ones[:],
+                    rhs=bias_rows[:, first + at : first + at + N_TILE],
+                    start=True,
+                    stop=True,
+                )
+            nc.scalar.copy(out=bias_all[:, first : first + cols], in_=spread[:])
+
         position = consts.tile([P, 1], F32)
         nc.vector.tensor_copy(out=position[:], in_=position_i[:])
         turns = consts.tile([P, 2, PACK, HALF_ROWS], F32)
@@ -187,7 +204,7 @@ def tile_deepseekmla_pa_kernel(tc, x, W_c, b_c, W_d, b_d, out):
             nc.vector.tensor_tensor(
                 out=c_f32[:, b],
                 in0=c_ps[:].rearrange("p (m t) -> p t m", t=PACK),
-                in1=bc_all[:].rearrange("p (m t) -> p t m", t=PACK),
+                in1=bc_all.rearrange("p (m t) -> p t m", t=PACK),
                 op=ALU.add,
             )
             first_half = slice(0, HALF_ROWS)
@@ -252,6 +269,9 @@ def tile_deepseekmla_pa_kernel(tc, x, W_c, b_c, W_d, b_d, out):
                 in_=wd_grouped[n][:].rearrange("p c j -> p (c j)"),
             )
 
+        broadcast_bias(D_OUT, DC)
+        broadcast_bias(0, BIAS_COLS)
+
         for step in range(B + R_LAG):
             if step < B:
                 quantise_x(step)
@@ -285,6 +305,9 @@ def tile_deepseekmla_pa_kernel(tc, x, W_c, b_c, W_d, b_d, out):
                     start=True,
                     stop=True,
                 )
+            bias_first = (n + 2) * N_TILE
+            if bias_first % BIAS_COLS == 0 and bias_first < D_OUT:
+                broadcast_bias(bias_first, BIAS_COLS)
             for b in range(B):
                 if b == B // 2 and n + 1 < CHUNKS:
                     quantise_wd(n + 1)

@@ -29,10 +29,10 @@ HALF_ROWS = HALF // PACK
 W_D_LOAD_COLS = 1024
 STORE_COLS = 512
 REGROUP_COLS = 256
-BIAS_COLS = 1024
 CHUNKS = D_OUT // N_TILE
 CHUNKS_PER_STORE = STORE_COLS // N_TILE
 PSUM_BANKS = 8
+OUT_BUFS = 16
 C_LAG = 2
 R_LAG = 3
 REGROUP_AHEAD = 2
@@ -58,7 +58,7 @@ def tile_deepseekmla_pa_kernel(tc, x, W_c, b_c, W_d, b_d, out):
         tc.tile_pool(name="x_stage", bufs=2) as x_stage,
         tc.tile_pool(name="w_stage", bufs=4) as w_stage,
         tc.tile_pool(name="rot_stage", bufs=2) as rot_stage,
-        tc.tile_pool(name="out_stage", bufs=2 * B) as out_stage,
+        tc.tile_pool(name="out_stage", bufs=OUT_BUFS) as out_stage,
         tc.psum_pool(name="psum", bufs=PSUM_BANKS) as psum,
         tc.manual_schedule(),
     ):
@@ -66,6 +66,11 @@ def tile_deepseekmla_pa_kernel(tc, x, W_c, b_c, W_d, b_d, out):
         wc_rows = W_c.rearrange("(g p j) c -> g p j c", p=P, j=PACK)
         for g in range(D_PASSES):
             nc.sync.dma_start(out=wc_raw[:, g], in_=wc_rows[g])
+        bias_cols = consts.tile([P, CHUNKS + 1, PACK], BF16)
+        nc.sync.dma_start(
+            out=bias_cols[:, 0:CHUNKS, :], in_=b_d.rearrange("(i q c) -> q i c", q=P, c=PACK)
+        )
+        nc.sync.dma_start(out=bias_cols[:, CHUNKS, :], in_=b_c.rearrange("(q c) -> q c", c=PACK))
         x_sb = keep.tile([P, B, D], BF16)
         for b in range(B):
             nc.sync.dma_start(out=x_sb[:, b, :], in_=x[b])
@@ -77,64 +82,75 @@ def tile_deepseekmla_pa_kernel(tc, x, W_c, b_c, W_d, b_d, out):
                 out=wd_raw[i][:], in_=wd_rows[:, :, i * W_D_LOAD_COLS : (i + 1) * W_D_LOAD_COLS]
             )
 
-        position_i = consts.tile([P, 1], I32)
-        nc.gpsimd.iota(position_i[:], pattern=[[0, 1]], base=0, channel_multiplier=1)
-        bias_rows = consts.tile([P, D_OUT + DC], BF16)
-        nc.gpsimd.memset(bias_rows[:].bitcast(F32), 0.0)
-        nc.scalar.dma_start(out=bias_rows[0:1, 0:D_OUT], in_=b_d.rearrange("(o n) -> o n", o=1))
-        nc.scalar.dma_start(out=bias_rows[0:1, D_OUT:], in_=b_c.rearrange("(o n) -> o n", o=1))
-        ones = consts.tile([P, P], BF16)
-        nc.gpsimd.memset(ones[:], 1.0)
+        position = consts.tile([P, 1], F32)
+        nc.gpsimd.iota(
+            position[:], pattern=[[0, 1]], base=0, channel_multiplier=1,
+            allow_small_or_imprecise_dtypes=True,
+        )
         ident = consts.tile([P, P], F32)
         make_identity(nc, ident[:])
-        bias_all = consts.tile([P, D_OUT + DC], BF16)
-        bd_all = bias_all[:, 0:D_OUT]
-        bc_all = bias_all[:, D_OUT:]
+        ident_bf16 = consts.tile([P, P], BF16)
+        make_identity(nc, ident_bf16[:])
 
-        def broadcast_bias(first, cols):
-            spread = psum.tile([P, cols], BF16, tag="bank")
-            for at in range(0, cols, N_TILE):
-                nc.tensor.matmul(
-                    out=spread[:, at : at + N_TILE],
-                    lhsT=ones[:],
-                    rhs=bias_rows[:, first + at : first + at + N_TILE],
-                    start=True,
-                    stop=True,
-                )
-            nc.scalar.copy(out=bias_all[:, first : first + cols], in_=spread[:])
-
-        position = consts.tile([P, 1], F32)
-        nc.vector.tensor_copy(out=position[:], in_=position_i[:])
+        sin_table_loaded = consts.tile([P, 1], F32)
+        nc.scalar.activation(out=sin_table_loaded[:], in_=position[:], func=ACT.Sin, scale=0.0)
         turns = consts.tile([P, 2, PACK, HALF_ROWS], F32)
         for j in range(HALF):
             turns_per_position = 1.0 / ROPE_BASE ** (2 * j / DR) / (2.0 * math.pi)
-            nc.vector.tensor_scalar_mul(
+            nc.scalar.mul(
                 out=turns[:, 0, j % PACK, j // PACK : j // PACK + 1],
-                in0=position[:],
-                scalar1=turns_per_position,
+                in_=position[:],
+                mul=turns_per_position,
             )
-        nc.vector.tensor_scalar_add(out=turns[:, 1], in0=turns[:, 0], scalar1=0.25)
+        nc.scalar.add(out=turns[:, 1], in_=turns[:, 0], add=0.25)
         whole_turns = consts.tile([P, 2, PACK, HALF_ROWS], F32)
-        nc.vector.tensor_scalar_add(out=whole_turns[:], in0=turns[:], scalar1=ROUND_MAGIC)
+        nc.scalar.add(out=whole_turns[:], in_=turns[:], add=ROUND_MAGIC)
         minus_part_turn = consts.tile([P, 2, PACK, HALF_ROWS], F32)
-        nc.vector.scalar_tensor_tensor(
-            out=minus_part_turn[:].rearrange("p s t m -> p (s t m)"),
-            in0=whole_turns[:].rearrange("p s t m -> p (s t m)"),
-            scalar=ROUND_MAGIC,
-            in1=turns[:].rearrange("p s t m -> p (s t m)"),
-            op0=ALU.subtract,
-            op1=ALU.subtract,
-        )
         sin_cos = consts.tile([P, 2, PACK, 2, HALF_ROWS], F32)
-        for h in range(2):
-            nc.scalar.activation(
-                out=sin_cos[:, :, :, h, :],
-                in_=minus_part_turn[:],
-                func=ACT.Sin,
-                scale=-2.0 * math.pi,
-            )
         sin_a = sin_cos[:, 0].rearrange("p t h m -> p t (h m)")
         cos_a = sin_cos[:, 1].rearrange("p t h m -> p t (h m)")
+
+        def finish_sin_cos():
+            nc.vector.scalar_tensor_tensor(
+                out=minus_part_turn[:].rearrange("p s t m -> p (s t m)"),
+                in0=whole_turns[:].rearrange("p s t m -> p (s t m)"),
+                scalar=ROUND_MAGIC,
+                in1=turns[:].rearrange("p s t m -> p (s t m)"),
+                op0=ALU.subtract,
+                op1=ALU.subtract,
+            )
+            for h in range(2):
+                nc.scalar.activation(
+                    out=sin_cos[:, :, :, h, :],
+                    in_=minus_part_turn[:],
+                    func=ACT.Sin,
+                    scale=-2.0 * math.pi,
+                )
+
+        bd_all = consts.tile([P, D_OUT], BF16)
+        bc_all = consts.tile([P, PACK, LATENT_ROWS], BF16)
+
+        def spread_bias(i):
+            spread = psum.tile([P, PACK, P], BF16, tag="bank")
+            for c in range(PACK):
+                nc.tensor.matmul(
+                    out=spread[:, c, :],
+                    lhsT=bias_cols[:, i, c : c + 1].to_broadcast([P, P]),
+                    rhs=ident_bf16[:],
+                    start=True,
+                    stop=True,
+                )
+            return spread
+
+        def spread_bd(n):
+            nc.scalar.copy(
+                out=bd_all[:, n * N_TILE : (n + 1) * N_TILE].rearrange("p (q c) -> p q c", c=PACK),
+                in_=spread_bias(n)[:].rearrange("p c q -> p q c"),
+            )
+
+        nc.scalar.copy(out=bc_all[:], in_=spread_bias(CHUNKS)[:])
+        for n in range(REGROUP_AHEAD):
+            spread_bd(n)
 
         wc_codes = keep.tile([P, D_PASSES, DC], U32, align_bytes=64)
         wc_scales = keep.tile([P, D_PASSES, DC], U8, align_bytes=64)
@@ -204,7 +220,7 @@ def tile_deepseekmla_pa_kernel(tc, x, W_c, b_c, W_d, b_d, out):
             nc.vector.tensor_tensor(
                 out=c_f32[:, b],
                 in0=c_ps[:].rearrange("p (m t) -> p t m", t=PACK),
-                in1=bc_all.rearrange("p (m t) -> p t m", t=PACK),
+                in1=bc_all[:],
                 op=ALU.add,
             )
             first_half = slice(0, HALF_ROWS)
@@ -269,12 +285,11 @@ def tile_deepseekmla_pa_kernel(tc, x, W_c, b_c, W_d, b_d, out):
                 in_=wd_grouped[n][:].rearrange("p c j -> p (c j)"),
             )
 
-        broadcast_bias(D_OUT, DC)
-        broadcast_bias(0, BIAS_COLS)
-
         for step in range(B + R_LAG):
             if step < B:
                 quantise_x(step)
+            if step == C_LAG:
+                finish_sin_cos()
             if C_LAG <= step < B + C_LAG:
                 compress_and_rotate(step - C_LAG)
             if step >= R_LAG:
@@ -289,6 +304,7 @@ def tile_deepseekmla_pa_kernel(tc, x, W_c, b_c, W_d, b_d, out):
             if n + REGROUP_AHEAD < CHUNKS:
                 for piece in range(PIECES):
                     regroup_wd(n + REGROUP_AHEAD, piece)
+                spread_bd(n + REGROUP_AHEAD)
             cols = slice(n * N_TILE, (n + 1) * N_TILE)
             place = (n % CHUNKS_PER_STORE) * N_TILE
             o_ps = {}
@@ -305,9 +321,6 @@ def tile_deepseekmla_pa_kernel(tc, x, W_c, b_c, W_d, b_d, out):
                     start=True,
                     stop=True,
                 )
-            bias_first = (n + 2) * N_TILE
-            if bias_first % BIAS_COLS == 0 and bias_first < D_OUT:
-                broadcast_bias(bias_first, BIAS_COLS)
             for b in range(B):
                 if b == B // 2 and n + 1 < CHUNKS:
                     quantise_wd(n + 1)

@@ -89,8 +89,6 @@ def tile_deepseekmla_pa_kernel(tc, x, W_c, b_c, W_d, b_d, out):
         )
         ident = consts.tile([P, P], F32)
         make_identity(nc, ident[:])
-        ident_bf16 = consts.tile([P, P], BF16)
-        make_identity(nc, ident_bf16[:])
 
         sin_table_loaded = consts.tile([P, 1], F32)
         nc.scalar.activation(out=sin_table_loaded[:], in_=position[:], func=ACT.Sin, scale=0.0)
@@ -127,30 +125,30 @@ def tile_deepseekmla_pa_kernel(tc, x, W_c, b_c, W_d, b_d, out):
                     scale=-2.0 * math.pi,
                 )
 
+        bias_words = bias_cols[:].rearrange("p i c -> p (i c)").bitcast(F32)
         bd_all = consts.tile([P, D_OUT], BF16)
-        bc_all = consts.tile([P, PACK, LATENT_ROWS], BF16)
+        bc_all = consts.tile([P, DC], BF16)
 
-        def spread_bias(i):
-            spread = psum.tile([P, PACK, P], BF16, tag="bank")
-            for c in range(PACK):
-                nc.tensor.matmul(
-                    out=spread[:, c, :],
-                    lhsT=bias_cols[:, i, c : c + 1].to_broadcast([P, P]),
-                    rhs=ident_bf16[:],
-                    start=True,
-                    stop=True,
-                )
-            return spread
-
-        def spread_bd(n):
+        def spread_bias(first, count, dest):
+            spread = psum.tile([P, count, 2, P], F32, tag="bank")
+            for i in range(count):
+                for u in range(2):
+                    w = 2 * (first + i) + u
+                    nc.tensor.transpose(
+                        out=spread[:, i, u, :],
+                        in_=bias_words[:, w : w + 1].to_broadcast([P, P]),
+                        identity=ident[:],
+                    )
             nc.scalar.copy(
-                out=bd_all[:, n * N_TILE : (n + 1) * N_TILE].rearrange("p (q c) -> p q c", c=PACK),
-                in_=spread_bias(n)[:].rearrange("p c q -> p q c"),
+                out=dest.bitcast(F32).rearrange("p (i q u) -> p i q u", i=count, u=2),
+                in_=spread[:].rearrange("p i u q -> p i q u"),
             )
 
-        nc.scalar.copy(out=bc_all[:], in_=spread_bias(CHUNKS)[:])
-        for n in range(REGROUP_AHEAD):
-            spread_bd(n)
+        def spread_bd(n):
+            spread_bias(n, 2, bd_all[:, n * N_TILE : (n + 2) * N_TILE])
+
+        spread_bias(CHUNKS, 1, bc_all[:])
+        spread_bd(0)
 
         wc_codes = keep.tile([P, D_PASSES, DC], U32, align_bytes=64)
         wc_scales = keep.tile([P, D_PASSES, DC], U8, align_bytes=64)
@@ -220,7 +218,7 @@ def tile_deepseekmla_pa_kernel(tc, x, W_c, b_c, W_d, b_d, out):
             nc.vector.tensor_tensor(
                 out=c_f32[:, b],
                 in0=c_ps[:].rearrange("p (m t) -> p t m", t=PACK),
-                in1=bc_all[:],
+                in1=bc_all[:].rearrange("p (m t) -> p t m", t=PACK),
                 op=ALU.add,
             )
             first_half = slice(0, HALF_ROWS)
@@ -304,7 +302,8 @@ def tile_deepseekmla_pa_kernel(tc, x, W_c, b_c, W_d, b_d, out):
             if n + REGROUP_AHEAD < CHUNKS:
                 for piece in range(PIECES):
                     regroup_wd(n + REGROUP_AHEAD, piece)
-                spread_bd(n + REGROUP_AHEAD)
+                if n % 2 == 0:
+                    spread_bd(n + REGROUP_AHEAD)
             cols = slice(n * N_TILE, (n + 1) * N_TILE)
             place = (n % CHUNKS_PER_STORE) * N_TILE
             o_ps = {}

@@ -26,18 +26,17 @@ LATENT_ROWS = DC // PACK
 ROT_ROWS = DR // PACK
 HALF_ROWS = HALF // PACK
 
-W_D_LOAD_COLS = 1024
-STORE_COLS = 512
+W_D_LOADS = [N_TILE] * 2 + [2 * N_TILE] * ((D_OUT // N_TILE - 2) // 2)
 REGROUP_COLS = 256
 CHUNKS = D_OUT // N_TILE
-CHUNKS_PER_STORE = STORE_COLS // N_TILE
+EARLY_CHUNKS = 2
 PSUM_BANKS = 8
 OUT_BUFS = 16
-C_LAG = 2
-R_LAG = 3
 REGROUP_AHEAD = 2
 PIECES = N_TILE // REGROUP_COLS
-assert B == REGROUP_AHEAD * PIECES
+BIAS_RUN = D_OUT // P
+BIAS_WORDS = BIAS_RUN // 2
+BIAS_WORDS_PER_BANK = N_TILE // P
 ROUND_MAGIC = 1.5 * 2.0**23
 
 FLOPS = 2 * B * S * D * DC + 2 * B * S * DC * D_OUT
@@ -55,32 +54,48 @@ def tile_deepseekmla_pa_kernel(tc, x, W_c, b_c, W_d, b_d, out):
     with (
         tc.tile_pool(name="consts", bufs=1) as consts,
         tc.tile_pool(name="keep", bufs=1) as keep,
-        tc.tile_pool(name="x_stage", bufs=2) as x_stage,
+        tc.tile_pool(name="x_stage", bufs=B) as x_stage,
         tc.tile_pool(name="w_stage", bufs=4) as w_stage,
         tc.tile_pool(name="rot_stage", bufs=2) as rot_stage,
         tc.tile_pool(name="out_stage", bufs=OUT_BUFS) as out_stage,
         tc.psum_pool(name="psum", bufs=PSUM_BANKS) as psum,
         tc.manual_schedule(),
     ):
+        bd_cols = consts.tile([P, BIAS_RUN], BF16)
+        nc.sync.dma_start(out=bd_cols[:], in_=b_d.rearrange("(q c) -> q c", q=P))
+        bc_cols = consts.tile([P, PACK], BF16)
+        nc.sync.dma_start(out=bc_cols[:], in_=b_c.rearrange("(q c) -> q c", q=P))
         wc_raw = keep.tile([P, D_PASSES, PACK, DC], BF16)
         wc_rows = W_c.rearrange("(g p j) c -> g p j c", p=P, j=PACK)
-        for g in range(D_PASSES):
-            nc.sync.dma_start(out=wc_raw[:, g], in_=wc_rows[g])
-        bias_cols = consts.tile([P, CHUNKS + 1, PACK], BF16)
-        nc.sync.dma_start(
-            out=bias_cols[:, 0:CHUNKS, :], in_=b_d.rearrange("(i q c) -> q i c", q=P, c=PACK)
-        )
-        nc.sync.dma_start(out=bias_cols[:, CHUNKS, :], in_=b_c.rearrange("(q c) -> q c", c=PACK))
         x_sb = keep.tile([P, B, D], BF16)
-        for b in range(B):
-            nc.sync.dma_start(out=x_sb[:, b, :], in_=x[b])
         wd_rows = W_d.rearrange("(p j) n -> p j n", j=PACK)
         wd_raw = []
-        for i in range(D_OUT // W_D_LOAD_COLS):
-            wd_raw.append(keep.tile([P, PACK, W_D_LOAD_COLS], BF16, name="wd_raw_%d" % i))
-            nc.sync.dma_start(
-                out=wd_raw[i][:], in_=wd_rows[:, :, i * W_D_LOAD_COLS : (i + 1) * W_D_LOAD_COLS]
-            )
+
+        def load_wc(g):
+            nc.sync.dma_start(out=wc_raw[:, g], in_=wc_rows[g])
+
+        def load_x(b):
+            nc.sync.dma_start(out=x_sb[:, b, :], in_=x[b])
+
+        def load_wd():
+            i = len(wd_raw)
+            first = sum(W_D_LOADS[:i])
+            width = W_D_LOADS[i]
+            raw = keep.tile([P, PACK, width], BF16, name="wd_raw_%d" % i)
+            wd_raw.append((first, raw))
+            nc.sync.dma_start(out=raw[:], in_=wd_rows[:, :, first : first + width])
+
+        load_wc(0)
+        load_wc(1)
+        load_x(0)
+        load_wc(2)
+        load_wd()
+        load_x(1)
+        load_wc(3)
+        load_x(2)
+        load_x(3)
+        for i in range(1, len(W_D_LOADS)):
+            load_wd()
 
         position = consts.tile([P, 1], F32)
         nc.gpsimd.iota(
@@ -93,13 +108,19 @@ def tile_deepseekmla_pa_kernel(tc, x, W_c, b_c, W_d, b_d, out):
         sin_table_loaded = consts.tile([P, 1], F32)
         nc.scalar.activation(out=sin_table_loaded[:], in_=position[:], func=ACT.Sin, scale=0.0)
         turns = consts.tile([P, 2, PACK, HALF_ROWS], F32)
-        for j in range(HALF):
-            turns_per_position = 1.0 / ROPE_BASE ** (2 * j / DR) / (2.0 * math.pi)
-            nc.scalar.mul(
-                out=turns[:, 0, j % PACK, j // PACK : j // PACK + 1],
-                in_=position[:],
-                mul=turns_per_position,
+        def step_down(out, in_, angles):
+            nc.vector.tensor_scalar(
+                out=out, in0=in_, scalar1=ROPE_BASE ** (-2 * angles / DR), scalar2=None, op0=ALU.mult
             )
+
+        nc.vector.tensor_scalar(
+            out=turns[:, 0, 0, 0:1], in0=position[:], scalar1=1.0 / (2.0 * math.pi), scalar2=None, op0=ALU.mult
+        )
+        step_down(turns[:, 0, 1, 0:1], turns[:, 0, 0, 0:1], 1)
+        step_down(turns[:, 0, 2:4, 0], turns[:, 0, 0:2, 0], 2)
+        step_down(turns[:, 0, :, 1], turns[:, 0, :, 0], 4)
+        step_down(turns[:, 0, :, 2:4], turns[:, 0, :, 0:2], 8)
+        step_down(turns[:, 0, :, 4:8], turns[:, 0, :, 0:4], 16)
         nc.scalar.add(out=turns[:, 1], in_=turns[:, 0], add=0.25)
         whole_turns = consts.tile([P, 2, PACK, HALF_ROWS], F32)
         nc.scalar.add(out=whole_turns[:], in_=turns[:], add=ROUND_MAGIC)
@@ -108,7 +129,7 @@ def tile_deepseekmla_pa_kernel(tc, x, W_c, b_c, W_d, b_d, out):
         sin_a = sin_cos[:, 0].rearrange("p t h m -> p t (h m)")
         cos_a = sin_cos[:, 1].rearrange("p t h m -> p t (h m)")
 
-        def finish_sin_cos():
+        def take_off_whole_turns():
             nc.vector.scalar_tensor_tensor(
                 out=minus_part_turn[:].rearrange("p s t m -> p (s t m)"),
                 in0=whole_turns[:].rearrange("p s t m -> p (s t m)"),
@@ -117,6 +138,8 @@ def tile_deepseekmla_pa_kernel(tc, x, W_c, b_c, W_d, b_d, out):
                 op0=ALU.subtract,
                 op1=ALU.subtract,
             )
+
+        def finish_sin_cos():
             for h in range(2):
                 nc.scalar.activation(
                     out=sin_cos[:, :, :, h, :],
@@ -125,30 +148,22 @@ def tile_deepseekmla_pa_kernel(tc, x, W_c, b_c, W_d, b_d, out):
                     scale=-2.0 * math.pi,
                 )
 
-        bias_words = bias_cols[:].rearrange("p i c -> p (i c)").bitcast(F32)
         bd_all = consts.tile([P, D_OUT], BF16)
         bc_all = consts.tile([P, DC], BF16)
 
-        def spread_bias(first, count, dest):
-            spread = psum.tile([P, count, 2, P], F32, tag="bank")
-            for i in range(count):
-                for u in range(2):
-                    w = 2 * (first + i) + u
-                    nc.tensor.transpose(
-                        out=spread[:, i, u, :],
-                        in_=bias_words[:, w : w + 1].to_broadcast([P, P]),
-                        identity=ident[:],
-                    )
+        def spread_bias(cols, first, count, words, dest):
+            spread = psum.tile([P, count, P], F32, tag="bank")
+            for u in range(count):
+                w = first + u
+                nc.tensor.transpose(
+                    out=spread[:, u, :],
+                    in_=cols[:].bitcast(F32)[:, w : w + 1].to_broadcast([P, P]),
+                    identity=ident[:],
+                )
             nc.scalar.copy(
-                out=dest.bitcast(F32).rearrange("p (i q u) -> p i q u", i=count, u=2),
-                in_=spread[:].rearrange("p i u q -> p i q u"),
+                out=dest[:].bitcast(F32).rearrange("p (q u) -> p q u", u=words)[:, :, first : first + count],
+                in_=spread[:].rearrange("p u q -> p q u"),
             )
-
-        def spread_bd(n):
-            spread_bias(n, 2, bd_all[:, n * N_TILE : (n + 2) * N_TILE])
-
-        spread_bias(CHUNKS, 1, bc_all[:])
-        spread_bd(0)
 
         wc_codes = keep.tile([P, D_PASSES, DC], U32, align_bytes=64)
         wc_scales = keep.tile([P, D_PASSES, DC], U8, align_bytes=64)
@@ -164,11 +179,8 @@ def tile_deepseekmla_pa_kernel(tc, x, W_c, b_c, W_d, b_d, out):
                 in_=wc_grouped[g][:].rearrange("p c j -> p (c j)"),
             )
 
-        for g in range(D_PASSES):
+        def regroup_wc(g):
             regroup_rows(nc.vector.tensor_copy, wc_grouped[g][:], wc_raw[:, g])
-            if g > 0:
-                quantise_wc(g - 1)
-        quantise_wc(D_PASSES - 1)
 
         x_codes = keep.tile([P, B, D_PASSES, S], U32, align_bytes=64)
         x_scales = keep.tile([P, B, D_PASSES, S], U8, align_bytes=64)
@@ -177,10 +189,17 @@ def tile_deepseekmla_pa_kernel(tc, x, W_c, b_c, W_d, b_d, out):
         r_codes = keep.tile([P, B, S], U32, align_bytes=64)
         r_scales = keep.tile([P, B, S], U8, align_bytes=64)
 
-        def quantise_x(b):
+        x_grouped = {}
+        c_ps = {}
+        times_cos = {}
+        times_sin = {}
+
+        def transpose_x(b):
             x_words = x_sb[:, b, :].bitcast(F32)
-            x_grouped = x_stage.tile([P, D_PASSES * S * PACK], BF16, align_bytes=64)
-            x_grouped_words = x_grouped[:].bitcast(F32).rearrange(
+            x_grouped[b] = x_stage.tile(
+                [P, D_PASSES * S * PACK], BF16, align_bytes=64, tag="x_grouped", name="x_grouped_%d" % b
+            )
+            x_grouped_words = x_grouped[b][:].bitcast(F32).rearrange(
                 "p (g r u) -> p g r u", g=D_PASSES, u=2
             )
             for g_pair in range(0, D_PASSES, 2):
@@ -197,17 +216,19 @@ def tile_deepseekmla_pa_kernel(tc, x, W_c, b_c, W_d, b_d, out):
                     out=x_grouped_words[:, g_pair : g_pair + 2],
                     in_=x_t[:].rearrange("p g u r -> p g r u"),
                 )
+
+        def quantise_x(b):
             nc.vector.quantize_mx(
                 out=x_codes[:, b].rearrange("p g r -> p (g r)").bitcast(FP8X4),
                 scales=x_scales[:, b].rearrange("p g r -> p (g r)"),
-                in_=x_grouped[:],
+                in_=x_grouped[b][:],
             )
 
-        def compress_and_rotate(b):
-            c_ps = psum.tile([P, DC], F32, tag="bank")
+        def compress(b):
+            c_ps[b] = psum.tile([P, DC], F32, tag="bank", name="c_ps_%d" % b)
             for g in range(D_PASSES):
                 nc.tensor.matmul_mx(
-                    out=c_ps[:],
+                    out=c_ps[b][:],
                     lhsT=x_codes[:, b, g, :].bitcast(FP8X4),
                     lhsT_scale=x_scales[:, b, g, :],
                     rhs=wc_codes[:, g, :].bitcast(FP8X4),
@@ -215,36 +236,43 @@ def tile_deepseekmla_pa_kernel(tc, x, W_c, b_c, W_d, b_d, out):
                     start=(g == 0),
                     stop=(g == D_PASSES - 1),
                 )
+
+        def add_bc(b):
             nc.vector.tensor_tensor(
                 out=c_f32[:, b],
-                in0=c_ps[:].rearrange("p (m t) -> p t m", t=PACK),
+                in0=c_ps[b][:].rearrange("p (m t) -> p t m", t=PACK),
                 in1=bc_all[:].rearrange("p (m t) -> p t m", t=PACK),
                 op=ALU.add,
             )
-            first_half = slice(0, HALF_ROWS)
-            second_half = slice(HALF_ROWS, ROT_ROWS)
-            times_cos = rot_stage.tile([P, PACK, ROT_ROWS], F32)
-            times_sin = rot_stage.tile([P, PACK, ROT_ROWS], F32)
+
+        first_half = slice(0, HALF_ROWS)
+        second_half = slice(HALF_ROWS, ROT_ROWS)
+
+        def rotate_products(b):
+            times_cos[b] = rot_stage.tile([P, PACK, ROT_ROWS], F32, tag="times_cos", name="times_cos_%d" % b)
+            times_sin[b] = rot_stage.tile([P, PACK, ROT_ROWS], F32, tag="times_sin", name="times_sin_%d" % b)
             nc.vector.tensor_tensor(
-                out=times_cos[:], in0=c_f32[:, b, :, 0:ROT_ROWS], in1=cos_a, op=ALU.mult
+                out=times_cos[b][:], in0=c_f32[:, b, :, 0:ROT_ROWS], in1=cos_a, op=ALU.mult
             )
             nc.vector.tensor_tensor(
-                out=times_sin[:], in0=c_f32[:, b, :, 0:ROT_ROWS], in1=sin_a, op=ALU.mult
+                out=times_sin[b][:], in0=c_f32[:, b, :, 0:ROT_ROWS], in1=sin_a, op=ALU.mult
             )
+
+        def rotate_sums(b):
             nc.vector.tensor_tensor(
                 out=c_f32[:, b, :, first_half],
-                in0=times_cos[:, :, first_half],
-                in1=times_sin[:, :, second_half],
+                in0=times_cos[b][:, :, first_half],
+                in1=times_sin[b][:, :, second_half],
                 op=ALU.subtract,
             )
             nc.vector.tensor_tensor(
                 out=c_f32[:, b, :, second_half],
-                in0=times_cos[:, :, second_half],
-                in1=times_sin[:, :, first_half],
+                in0=times_cos[b][:, :, second_half],
+                in1=times_sin[b][:, :, first_half],
                 op=ALU.add,
             )
 
-        def quantise_r(b):
+        def transpose_r(b):
             r_t = psum.tile([P, PACK, S], F32, tag="bank")
             for t in range(PACK):
                 nc.tensor.transpose(out=r_t[:, t, :], in_=c_f32[:, b, t, :], identity=ident[:])
@@ -252,6 +280,8 @@ def tile_deepseekmla_pa_kernel(tc, x, W_c, b_c, W_d, b_d, out):
                 out=r_grouped[:, b, :].rearrange("p (r t) -> p r t", t=PACK),
                 in_=r_t[:].rearrange("p t r -> p r t"),
             )
+
+        def quantise_r(b):
             nc.vector.quantize_mx(
                 out=r_codes[:, b, :].bitcast(FP8X4),
                 scales=r_scales[:, b, :],
@@ -268,11 +298,12 @@ def tile_deepseekmla_pa_kernel(tc, x, W_c, b_c, W_d, b_d, out):
                     [P, N_TILE, PACK], BF16, align_bytes=64, tag="w_grouped", name="wd_grouped_%d" % n
                 )
             to = piece * REGROUP_COLS
-            load, place = divmod(n * N_TILE + to, W_D_LOAD_COLS)
+            first, raw = [load for load in wd_raw if load[0] <= n * N_TILE][-1]
+            place = n * N_TILE + to - first
             regroup_rows(
                 nc.scalar.copy,
                 wd_grouped[n][:, to : to + REGROUP_COLS, :],
-                wd_raw[load][:, :, place : place + REGROUP_COLS],
+                raw[:, :, place : place + REGROUP_COLS],
             )
 
         def quantise_wd(n):
@@ -283,54 +314,112 @@ def tile_deepseekmla_pa_kernel(tc, x, W_c, b_c, W_d, b_d, out):
                 in_=wd_grouped[n][:].rearrange("p c j -> p (c j)"),
             )
 
-        for step in range(B + R_LAG):
-            if step < B:
-                quantise_x(step)
-            if step == C_LAG:
-                finish_sin_cos()
-            if C_LAG <= step < B + C_LAG:
-                compress_and_rotate(step - C_LAG)
-            if step >= R_LAG:
-                quantise_r(step - R_LAG)
-                n, piece = divmod(step - R_LAG, PIECES)
-                regroup_wd(n, piece)
-                if (n, piece) == (1, 0):
-                    quantise_wd(0)
+        o_ps = {}
 
-        out_sb = {}
-        for n in range(CHUNKS):
-            if n + REGROUP_AHEAD < CHUNKS:
-                for piece in range(PIECES):
-                    regroup_wd(n + REGROUP_AHEAD, piece)
-                if n % 2 == 0:
-                    spread_bd(n + REGROUP_AHEAD)
+        def multiply(n, b):
             cols = slice(n * N_TILE, (n + 1) * N_TILE)
-            place = (n % CHUNKS_PER_STORE) * N_TILE
-            o_ps = {}
+            o_ps[n, b] = psum.tile([P, N_TILE], F32, tag="bank", name="o_ps_%d_%d" % (n, b))
+            nc.tensor.matmul_mx(
+                out=o_ps[n, b][:],
+                lhsT=r_codes[:, b, :].bitcast(FP8X4),
+                lhsT_scale=r_scales[:, b, :],
+                rhs=wd_codes[:, cols].bitcast(FP8X4),
+                rhs_scale=wd_scales[:, cols],
+                start=True,
+                stop=True,
+            )
+
+        def finish(n, b):
+            cols = slice(n * N_TILE, (n + 1) * N_TILE)
+            out_sb = out_stage.tile([P, N_TILE], F32, tag="out_sb", name="out_sb_%d_%d" % (n, b))
+            nc.vector.tensor_tensor(
+                out=out_sb[:], in0=o_ps[n, b][:], in1=bd_all[:, cols], op=ALU.add
+            )
+            nc.sync.dma_start(out=out[b, :, cols], in_=out_sb[:])
+
+        def regroup_chunk(n):
+            for piece in range(PIECES):
+                regroup_wd(n, piece)
+
+        spread_bias(bc_cols, 0, PACK // 2, PACK // 2, bc_all)
+        for first in range(0, BIAS_WORDS, BIAS_WORDS_PER_BANK):
+            spread_bias(bd_cols, first, BIAS_WORDS_PER_BANK, BIAS_WORDS, bd_all)
+
+        regroup_wc(0)
+        take_off_whole_turns()
+        transpose_x(0)
+        finish_sin_cos()
+        regroup_chunk(0)
+        regroup_wc(1)
+        quantise_wc(0)
+        quantise_wc(1)
+        regroup_wc(2)
+        quantise_x(0)
+        quantise_wc(2)
+        regroup_wc(3)
+        transpose_x(1)
+        transpose_x(2)
+        quantise_wd(0)
+        quantise_wc(3)
+        quantise_x(1)
+
+        compress(0)
+        transpose_x(3)
+        regroup_wd(1, 0)
+        quantise_x(2)
+        compress(1)
+        add_bc(0)
+        compress(2)
+        quantise_x(3)
+        rotate_products(0)
+        add_bc(1)
+        rotate_sums(0)
+        transpose_r(0)
+        compress(3)
+        regroup_wd(1, 1)
+        rotate_products(1)
+        add_bc(2)
+        rotate_sums(1)
+        transpose_r(1)
+        rotate_products(2)
+        quantise_r(0)
+        rotate_sums(2)
+        transpose_r(2)
+        add_bc(3)
+        multiply(0, 0)
+        quantise_r(1)
+        rotate_products(3)
+        finish(0, 0)
+        rotate_sums(3)
+        quantise_wd(1)
+        multiply(0, 1)
+        transpose_r(3)
+        multiply(1, 0)
+        multiply(1, 1)
+        finish(0, 1)
+        quantise_r(2)
+        finish(1, 0)
+        multiply(0, 2)
+        multiply(1, 2)
+        finish(1, 1)
+        regroup_wd(2, 0)
+        quantise_r(3)
+        finish(0, 2)
+        multiply(0, 3)
+        multiply(1, 3)
+        regroup_wd(2, 1)
+        finish(1, 2)
+        regroup_chunk(3)
+        quantise_wd(2)
+        finish(0, 3)
+        finish(1, 3)
+
+        for n in range(EARLY_CHUNKS, CHUNKS):
+            if n + REGROUP_AHEAD < CHUNKS:
+                regroup_chunk(n + REGROUP_AHEAD)
             for b in range(B):
-                if place == 0:
-                    out_sb[b] = out_stage.tile([P, STORE_COLS], F32, tag="out_sb", name="out_sb_%d" % b)
-                o_ps[b] = psum.tile([P, N_TILE], F32, tag="bank", name="o_ps_%d" % b)
-                nc.tensor.matmul_mx(
-                    out=o_ps[b][:],
-                    lhsT=r_codes[:, b, :].bitcast(FP8X4),
-                    lhsT_scale=r_scales[:, b, :],
-                    rhs=wd_codes[:, cols].bitcast(FP8X4),
-                    rhs_scale=wd_scales[:, cols],
-                    start=True,
-                    stop=True,
-                )
+                multiply(n, b)
             for b in range(B):
                 if b == B // 2 and n + 1 < CHUNKS:
                     quantise_wd(n + 1)
-                nc.vector.tensor_tensor(
-                    out=out_sb[b][:, place : place + N_TILE],
-                    in0=o_ps[b][:],
-                    in1=bd_all[:, cols],
-                    op=ALU.add,
-                )
-                if place + N_TILE == STORE_COLS:
-                    store_first = (n + 1) * N_TILE - STORE_COLS
-                    nc.sync.dma_start(
-                        out=out[b, :, store_first : store_first + STORE_COLS], in_=out_sb[b][:]
-                    )
+                finish(n, b)

@@ -29,12 +29,11 @@ HALF_ROWS = HALF // PACK
 W_D_LOADS = [N_TILE] * 2 + [2 * N_TILE] * ((D_OUT // N_TILE - 2) // 2)
 REGROUP_COLS = 256
 CHUNKS = D_OUT // N_TILE
-EARLY_CHUNKS = 2
 PSUM_BANKS = 8
-OUT_BUFS = 16
-REGROUP_AHEAD = 2
+OUT_BUFS = 9
 PIECES = N_TILE // REGROUP_COLS
-BIAS_RUN = D_OUT // P
+BIAS_PARTS = 2
+BIAS_RUN = D_OUT // BIAS_PARTS // P
 BIAS_WORDS = BIAS_RUN // 2
 BIAS_WORDS_PER_BANK = N_TILE // P
 ROUND_MAGIC = 1.5 * 2.0**23
@@ -61,8 +60,8 @@ def tile_deepseekmla_pa_kernel(tc, x, W_c, b_c, W_d, b_d, out):
         tc.psum_pool(name="psum", bufs=PSUM_BANKS) as psum,
         tc.manual_schedule(),
     ):
-        bd_cols = consts.tile([P, BIAS_RUN], BF16)
-        nc.sync.dma_start(out=bd_cols[:], in_=b_d.rearrange("(q c) -> q c", q=P))
+        bd_cols = consts.tile([P, BIAS_PARTS, BIAS_RUN], BF16)
+        nc.sync.dma_start(out=bd_cols[:], in_=b_d.rearrange("(h q c) -> q h c", h=BIAS_PARTS, q=P))
         bc_cols = consts.tile([P, PACK], BF16)
         nc.sync.dma_start(out=bc_cols[:], in_=b_c.rearrange("(q c) -> q c", q=P))
         wc_raw = keep.tile([P, D_PASSES, PACK, DC], BF16)
@@ -157,12 +156,22 @@ def tile_deepseekmla_pa_kernel(tc, x, W_c, b_c, W_d, b_d, out):
                 w = first + u
                 nc.tensor.transpose(
                     out=spread[:, u, :],
-                    in_=cols[:].bitcast(F32)[:, w : w + 1].to_broadcast([P, P]),
+                    in_=cols.bitcast(F32)[:, w : w + 1].to_broadcast([P, P]),
                     identity=ident[:],
                 )
             nc.scalar.copy(
-                out=dest[:].bitcast(F32).rearrange("p (q u) -> p q u", u=words)[:, :, first : first + count],
+                out=dest.bitcast(F32).rearrange("p (q u) -> p q u", u=words)[:, :, first : first + count],
                 in_=spread[:].rearrange("p u q -> p q u"),
+            )
+
+        def spread_bd(part, bank):
+            half = D_OUT // BIAS_PARTS
+            spread_bias(
+                bd_cols[:, part, :],
+                bank * BIAS_WORDS_PER_BANK,
+                BIAS_WORDS_PER_BANK,
+                BIAS_WORDS,
+                bd_all[:, part * half : (part + 1) * half],
             )
 
         wc_codes = keep.tile([P, D_PASSES, DC], U32, align_bytes=64)
@@ -224,9 +233,10 @@ def tile_deepseekmla_pa_kernel(tc, x, W_c, b_c, W_d, b_d, out):
                 in_=x_grouped[b][:],
             )
 
-        def compress(b):
-            c_ps[b] = psum.tile([P, DC], F32, tag="bank", name="c_ps_%d" % b)
-            for g in range(D_PASSES):
+        def compress(b, passes=range(D_PASSES)):
+            if passes[0] == 0:
+                c_ps[b] = psum.tile([P, DC], F32, tag="bank", name="c_ps_%d" % b)
+            for g in passes:
                 nc.tensor.matmul_mx(
                     out=c_ps[b][:],
                     lhsT=x_codes[:, b, g, :].bitcast(FP8X4),
@@ -315,6 +325,7 @@ def tile_deepseekmla_pa_kernel(tc, x, W_c, b_c, W_d, b_d, out):
             )
 
         o_ps = {}
+        out_sb = {}
 
         def multiply(n, b):
             cols = slice(n * N_TILE, (n + 1) * N_TILE)
@@ -331,95 +342,111 @@ def tile_deepseekmla_pa_kernel(tc, x, W_c, b_c, W_d, b_d, out):
 
         def finish(n, b):
             cols = slice(n * N_TILE, (n + 1) * N_TILE)
-            out_sb = out_stage.tile([P, N_TILE], F32, tag="out_sb", name="out_sb_%d_%d" % (n, b))
+            half = n % 2
+            if half == 0:
+                out_sb[b] = out_stage.tile([P, 2, N_TILE], F32, tag="out_sb", name="out_sb_%d_%d" % (n, b))
             nc.vector.tensor_tensor(
-                out=out_sb[:], in0=o_ps[n, b][:], in1=bd_all[:, cols], op=ALU.add
+                out=out_sb[b][:, half, :], in0=o_ps[n, b][:], in1=bd_all[:, cols], op=ALU.add
             )
-            nc.sync.dma_start(out=out[b, :, cols], in_=out_sb[:])
+            if n >= CHUNKS - 2:
+                nc.sync.dma_start(out=out[b, :, cols], in_=out_sb[b][:, half, :])
+            elif half == 1:
+                nc.sync.dma_start(
+                    out=out[b, :, (n - 1) * N_TILE : (n + 1) * N_TILE],
+                    in_=out_sb[b][:].rearrange("p h c -> p (h c)"),
+                )
+
+        def multiply_pair(n, b):
+            multiply(n, b)
+            multiply(n + 1, b)
 
         def regroup_chunk(n):
             for piece in range(PIECES):
                 regroup_wd(n, piece)
 
-        spread_bias(bc_cols, 0, PACK // 2, PACK // 2, bc_all)
-        for first in range(0, BIAS_WORDS, BIAS_WORDS_PER_BANK):
-            spread_bias(bd_cols, first, BIAS_WORDS_PER_BANK, BIAS_WORDS, bd_all)
+        spread_bias(bc_cols[:], 0, PACK // 2, PACK // 2, bc_all[:])
+        for bank in range(BIAS_WORDS // BIAS_WORDS_PER_BANK):
+            spread_bd(0, bank)
 
+        transpose_x(0)
         regroup_wc(0)
         take_off_whole_turns()
-        transpose_x(0)
         finish_sin_cos()
-        regroup_chunk(0)
         regroup_wc(1)
         quantise_wc(0)
         quantise_wc(1)
         regroup_wc(2)
         quantise_x(0)
         quantise_wc(2)
-        regroup_wc(3)
+        compress(0, range(D_PASSES - 1))
+        regroup_chunk(0)
         transpose_x(1)
+        regroup_wc(3)
         transpose_x(2)
+        transpose_x(3)
         quantise_wd(0)
         quantise_wc(3)
         quantise_x(1)
+        compress(0, range(D_PASSES - 1, D_PASSES))
 
-        compress(0)
-        transpose_x(3)
-        regroup_wd(1, 0)
-        quantise_x(2)
+        regroup_chunk(1)
         compress(1)
+        quantise_x(2)
         add_bc(0)
-        compress(2)
         quantise_x(3)
         rotate_products(0)
         add_bc(1)
         rotate_sums(0)
+        compress(2)
         transpose_r(0)
-        compress(3)
-        regroup_wd(1, 1)
+        regroup_wd(2, 0)
         rotate_products(1)
-        add_bc(2)
+        quantise_wd(1)
         rotate_sums(1)
+        compress(3)
         transpose_r(1)
+        regroup_wd(2, 1)
+        add_bc(2)
         rotate_products(2)
         quantise_r(0)
+        multiply_pair(0, 0)
         rotate_sums(2)
         transpose_r(2)
         add_bc(3)
-        multiply(0, 0)
         quantise_r(1)
         rotate_products(3)
         finish(0, 0)
         rotate_sums(3)
-        quantise_wd(1)
-        multiply(0, 1)
         transpose_r(3)
-        multiply(1, 0)
-        multiply(1, 1)
+        regroup_wd(3, 0)
+        multiply_pair(0, 1)
+        finish(1, 0)
         finish(0, 1)
         quantise_r(2)
-        finish(1, 0)
-        multiply(0, 2)
-        multiply(1, 2)
+        multiply_pair(0, 2)
+        regroup_wd(3, 1)
         finish(1, 1)
-        regroup_wd(2, 0)
-        quantise_r(3)
-        finish(0, 2)
-        multiply(0, 3)
-        multiply(1, 3)
-        regroup_wd(2, 1)
-        finish(1, 2)
-        regroup_chunk(3)
         quantise_wd(2)
+        finish(0, 2)
+        quantise_r(3)
+        multiply_pair(0, 3)
+        finish(1, 2)
         finish(0, 3)
+        quantise_wd(3)
         finish(1, 3)
 
-        for n in range(EARLY_CHUNKS, CHUNKS):
-            if n + REGROUP_AHEAD < CHUNKS:
-                regroup_chunk(n + REGROUP_AHEAD)
+        for n in range(2, CHUNKS, 2):
+            more = n + 2 < CHUNKS
+            if more:
+                for m in (n + 2, n + 3):
+                    regroup_chunk(m)
+                    bank = m - 5
+                    if bank in range(BIAS_WORDS // BIAS_WORDS_PER_BANK):
+                        spread_bd(1, bank)
             for b in range(B):
-                multiply(n, b)
+                multiply_pair(n, b)
             for b in range(B):
-                if b == B // 2 and n + 1 < CHUNKS:
-                    quantise_wd(n + 1)
+                if more and b >= B - 2:
+                    quantise_wd(n + b)
                 finish(n, b)
+                finish(n + 1, b)

@@ -407,20 +407,20 @@ def tile_deepseekmla_pa_kernel(tc, x, W_c, b_c, W_d, b_d, out):
         transpose_r(1)
         regroup_wd(2, 1)
         add_bc(2)
-        rotate_products(2)
         quantise_r(0)
         multiply_pair(0, 0)
+        rotate_products(2)
+        add_bc(3)
         rotate_sums(2)
         transpose_r(2)
-        add_bc(3)
-        quantise_r(1)
-        rotate_products(3)
         finish(0, 0)
+        quantise_r(1)
+        multiply_pair(0, 1)
+        rotate_products(3)
+        finish(1, 0)
         rotate_sums(3)
         transpose_r(3)
         regroup_wd(3, 0)
-        multiply_pair(0, 1)
-        finish(1, 0)
         finish(0, 1)
         quantise_r(2)
         multiply_pair(0, 2)
@@ -435,18 +435,24 @@ def tile_deepseekmla_pa_kernel(tc, x, W_c, b_c, W_d, b_d, out):
         quantise_wd(3)
         finish(1, 3)
 
-        for n in range(2, CHUNKS, 2):
-            more = n + 2 < CHUNKS
-            if more:
-                for m in (n + 2, n + 3):
-                    regroup_chunk(m)
-                    bank = m - 5
-                    if bank in range(BIAS_WORDS // BIAS_WORDS_PER_BANK):
-                        spread_bd(1, bank)
+        for n in range(2, CHUNKS - 2, 2):
+            for m in (n + 2, n + 3):
+                regroup_chunk(m)
+                bank = m - 5
+                if bank in range(BIAS_WORDS // BIAS_WORDS_PER_BANK):
+                    spread_bd(1, bank)
             for b in range(B):
                 multiply_pair(n, b)
             for b in range(B):
-                if more and b >= B - 2:
+                if b >= B - 2 and n + b < CHUNKS - 1:
                     quantise_wd(n + b)
                 finish(n, b)
                 finish(n + 1, b)
+
+        for n in range(CHUNKS - 2, CHUNKS):
+            for b in range(B):
+                multiply(n, b)
+            for b in range(B):
+                if b == B // 2 and n + 1 < CHUNKS:
+                    quantise_wd(n + 1)
+                finish(n, b)

@@ -64,8 +64,8 @@ def tile_deepseekmla_pa_kernel(tc, x, W_c, b_c, W_d, b_d, out):
         nc.sync.dma_start(out=bd_cols[:], in_=b_d.rearrange("(h q c) -> q h c", h=BIAS_PARTS, q=P))
         bc_cols = consts.tile([P, PACK], BF16)
         nc.sync.dma_start(out=bc_cols[:], in_=b_c.rearrange("(q c) -> q c", q=P))
-        wc_raw = keep.tile([P, D_PASSES, PACK, DC], BF16)
-        wc_rows = W_c.rearrange("(g p j) c -> g p j c", p=P, j=PACK)
+        wc_raw = keep.tile([P, D_PASSES, 2, 2, DC], BF16)
+        wc_rows = W_c.rearrange("(g u p e) c -> g p u e c", u=2, p=P, e=2)
         x_sb = keep.tile([P, B, D], BF16)
         wd_rows = W_d.rearrange("(p j) n -> p j n", j=PACK)
         wd_raw = []
@@ -189,7 +189,9 @@ def tile_deepseekmla_pa_kernel(tc, x, W_c, b_c, W_d, b_d, out):
             )
 
         def regroup_wc(g):
-            regroup_rows(nc.vector.tensor_copy, wc_grouped[g][:], wc_raw[:, g])
+            regroup_rows(
+                nc.vector.tensor_copy, wc_grouped[g][:], wc_raw[:, g].rearrange("p u e c -> p (u e) c")
+            )
 
         x_codes = keep.tile([P, B, D_PASSES, S], U32, align_bytes=64)
         x_scales = keep.tile([P, B, D_PASSES, S], U8, align_bytes=64)
@@ -214,11 +216,11 @@ def tile_deepseekmla_pa_kernel(tc, x, W_c, b_c, W_d, b_d, out):
             for g_pair in range(0, D_PASSES, 2):
                 x_t = psum.tile([P, 2, 2, S], F32, tag="bank")
                 for g in range(2):
-                    first_word = (g_pair + g) * (K_PASS // 2)
                     for u in range(2):
+                        first_word = (g_pair + g) * (K_PASS // 2) + u * P
                         nc.tensor.transpose(
                             out=x_t[:, g, u, :],
-                            in_=x_words[:, first_word + u : first_word + K_PASS // 2 : 2],
+                            in_=x_words[:, first_word : first_word + P],
                             identity=ident[:],
                         )
                 nc.scalar.copy(

@@ -205,6 +205,13 @@ def tile_deepseekmla_pa_kernel(tc, x, W_c, b_c, W_d, b_d, out):
         times_cos = {}
         times_sin = {}
 
+        def keep_clock_up(count):
+            for i in range(count):
+                unread = psum.tile([P, DC], F32, tag="bank", name="unread")
+                nc.tensor.matmul(
+                    out=unread[:], lhsT=wc_raw[:, 0, 0, 0, 0:P], rhs=wc_raw[:, 0, 0, 0, :], start=True, stop=True
+                )
+
         def transpose_x(b):
             x_words = x_sb[:, b, :].bitcast(F32)
             x_grouped[b] = x_stage.tile(
@@ -371,6 +378,7 @@ def tile_deepseekmla_pa_kernel(tc, x, W_c, b_c, W_d, b_d, out):
             spread_bd(0, bank)
 
         transpose_x(0)
+        keep_clock_up(4)
         regroup_wc(0)
         take_off_whole_turns()
         finish_sin_cos()
@@ -383,8 +391,10 @@ def tile_deepseekmla_pa_kernel(tc, x, W_c, b_c, W_d, b_d, out):
         compress(0, range(D_PASSES - 1))
         regroup_chunk(0)
         transpose_x(1)
+        keep_clock_up(1)
         regroup_wc(3)
         transpose_x(2)
+        keep_clock_up(1)
         transpose_x(3)
         quantise_wd(0)
         quantise_wc(3)

@@ -22,9 +22,6 @@ D_OUT = 3 * D
 HALF = DR // 2
 ROPE_BASE = 10000.0
 D_PASSES = D // K_PASS
-LATENT_ROWS = DC // PACK
-ROT_ROWS = DR // PACK
-HALF_ROWS = HALF // PACK
 
 W_D_LOADS = [N_TILE] * 2 + [2 * N_TILE] * ((D_OUT // N_TILE - 2) // 2)
 REGROUP_COLS = 256
@@ -60,10 +57,6 @@ def tile_deepseekmla_pa_kernel(tc, x, W_c, b_c, W_d, b_d, out):
         tc.psum_pool(name="psum", bufs=PSUM_BANKS) as psum,
         tc.manual_schedule(),
     ):
-        bd_cols = consts.tile([P, BIAS_PARTS, BIAS_RUN], BF16)
-        nc.sync.dma_start(out=bd_cols[:], in_=b_d.rearrange("(h q c) -> q h c", h=BIAS_PARTS, q=P))
-        bc_cols = consts.tile([P, PACK], BF16)
-        nc.sync.dma_start(out=bc_cols[:], in_=b_c.rearrange("(q c) -> q c", q=P))
         wc_raw = keep.tile([P, D_PASSES, 2, 2, DC], BF16)
         wc_rows = W_c.rearrange("(g u p e) c -> g p u e c", u=2, p=P, e=2)
         x_sb = keep.tile([P, B, D], BF16)
@@ -85,12 +78,16 @@ def tile_deepseekmla_pa_kernel(tc, x, W_c, b_c, W_d, b_d, out):
             nc.sync.dma_start(out=raw[:], in_=wd_rows[:, :, first : first + width])
 
         load_wc(0)
+        bd_cols = consts.tile([P, BIAS_PARTS, BIAS_RUN], BF16)
+        nc.sync.dma_start(out=bd_cols[:], in_=b_d.rearrange("(h q c) -> q h c", h=BIAS_PARTS, q=P))
+        bc_cols = consts.tile([P, PACK], BF16)
+        nc.sync.dma_start(out=bc_cols[:], in_=b_c.rearrange("(q c) -> q c", q=P))
         load_wc(1)
         load_x(0)
         load_wc(2)
         load_wd()
-        load_x(1)
         load_wc(3)
+        load_x(1)
         load_x(2)
         load_x(3)
         for i in range(1, len(W_D_LOADS)):
@@ -106,34 +103,30 @@ def tile_deepseekmla_pa_kernel(tc, x, W_c, b_c, W_d, b_d, out):
 
         sin_table_loaded = consts.tile([P, 1], F32)
         nc.scalar.activation(out=sin_table_loaded[:], in_=position[:], func=ACT.Sin, scale=0.0)
-        turns = consts.tile([P, 2, PACK, HALF_ROWS], F32)
-        def step_down(out, in_, angles):
-            nc.vector.tensor_scalar(
-                out=out, in0=in_, scalar1=ROPE_BASE ** (-2 * angles / DR), scalar2=None, op0=ALU.mult
-            )
-
+        turns = consts.tile([P, 2, HALF], F32)
         nc.vector.tensor_scalar(
-            out=turns[:, 0, 0, 0:1], in0=position[:], scalar1=1.0 / (2.0 * math.pi), scalar2=None, op0=ALU.mult
+            out=turns[:, 0, 0:1], in0=position[:], scalar1=1.0 / (2.0 * math.pi), scalar2=None, op0=ALU.mult
         )
-        step_down(turns[:, 0, 1, 0:1], turns[:, 0, 0, 0:1], 1)
-        step_down(turns[:, 0, 2:4, 0], turns[:, 0, 0:2, 0], 2)
-        step_down(turns[:, 0, :, 1], turns[:, 0, :, 0], 4)
-        step_down(turns[:, 0, :, 2:4], turns[:, 0, :, 0:2], 8)
-        step_down(turns[:, 0, :, 4:8], turns[:, 0, :, 0:4], 16)
+        for made in (1, 2, 4, 8, 16):
+            nc.vector.tensor_scalar(
+                out=turns[:, 0, made : 2 * made],
+                in0=turns[:, 0, 0:made],
+                scalar1=ROPE_BASE ** (-2 * made / DR),
+                scalar2=None,
+                op0=ALU.mult,
+            )
         nc.scalar.add(out=turns[:, 1], in_=turns[:, 0], add=0.25)
-        whole_turns = consts.tile([P, 2, PACK, HALF_ROWS], F32)
+        whole_turns = consts.tile([P, 2, HALF], F32)
         nc.scalar.add(out=whole_turns[:], in_=turns[:], add=ROUND_MAGIC)
-        minus_part_turn = consts.tile([P, 2, PACK, HALF_ROWS], F32)
-        sin_cos = consts.tile([P, 2, PACK, 2, HALF_ROWS], F32)
-        sin_a = sin_cos[:, 0].rearrange("p t h m -> p t (h m)")
-        cos_a = sin_cos[:, 1].rearrange("p t h m -> p t (h m)")
+        minus_part_turn = consts.tile([P, 2, HALF], F32)
+        sin_cos = consts.tile([P, 2, 2, HALF], F32)
 
         def take_off_whole_turns():
             nc.vector.scalar_tensor_tensor(
-                out=minus_part_turn[:].rearrange("p s t m -> p (s t m)"),
-                in0=whole_turns[:].rearrange("p s t m -> p (s t m)"),
+                out=minus_part_turn[:].rearrange("p s j -> p (s j)"),
+                in0=whole_turns[:].rearrange("p s j -> p (s j)"),
                 scalar=ROUND_MAGIC,
-                in1=turns[:].rearrange("p s t m -> p (s t m)"),
+                in1=turns[:].rearrange("p s j -> p (s j)"),
                 op0=ALU.subtract,
                 op1=ALU.subtract,
             )
@@ -141,7 +134,7 @@ def tile_deepseekmla_pa_kernel(tc, x, W_c, b_c, W_d, b_d, out):
         def finish_sin_cos():
             for h in range(2):
                 nc.scalar.activation(
-                    out=sin_cos[:, :, :, h, :],
+                    out=sin_cos[:, :, h, :],
                     in_=minus_part_turn[:],
                     func=ACT.Sin,
                     scale=-2.0 * math.pi,
@@ -195,13 +188,14 @@ def tile_deepseekmla_pa_kernel(tc, x, W_c, b_c, W_d, b_d, out):
 
         x_codes = keep.tile([P, B, D_PASSES, S], U32, align_bytes=64)
         x_scales = keep.tile([P, B, D_PASSES, S], U8, align_bytes=64)
-        c_f32 = keep.tile([P, B, PACK, LATENT_ROWS], F32)
+        r_rows = keep.tile([P, B, DC], BF16)
         r_grouped = keep.tile([P, B, S * PACK], BF16, align_bytes=64)
         r_codes = keep.tile([P, B, S], U32, align_bytes=64)
         r_scales = keep.tile([P, B, S], U8, align_bytes=64)
 
         x_grouped = {}
         c_ps = {}
+        c_rot = {}
         times_cos = {}
         times_sin = {}
 
@@ -257,47 +251,39 @@ def tile_deepseekmla_pa_kernel(tc, x, W_c, b_c, W_d, b_d, out):
                 )
 
         def add_bc(b):
+            c_rot[b] = rot_stage.tile([P, 2, HALF], F32, tag="c_rot", name="c_rot_%d" % b)
             nc.vector.tensor_tensor(
-                out=c_f32[:, b],
-                in0=c_ps[b][:].rearrange("p (m t) -> p t m", t=PACK),
-                in1=bc_all[:].rearrange("p (m t) -> p t m", t=PACK),
+                out=c_rot[b][:].rearrange("p h j -> p (h j)"),
+                in0=c_ps[b][:, 0:DR],
+                in1=bc_all[:, 0:DR],
                 op=ALU.add,
             )
-
-        first_half = slice(0, HALF_ROWS)
-        second_half = slice(HALF_ROWS, ROT_ROWS)
+            nc.vector.tensor_tensor(
+                out=r_rows[:, b, DR:DC], in0=c_ps[b][:, DR:DC], in1=bc_all[:, DR:DC], op=ALU.add
+            )
 
         def rotate_products(b):
-            times_cos[b] = rot_stage.tile([P, PACK, ROT_ROWS], F32, tag="times_cos", name="times_cos_%d" % b)
-            times_sin[b] = rot_stage.tile([P, PACK, ROT_ROWS], F32, tag="times_sin", name="times_sin_%d" % b)
-            nc.vector.tensor_tensor(
-                out=times_cos[b][:], in0=c_f32[:, b, :, 0:ROT_ROWS], in1=cos_a, op=ALU.mult
-            )
-            nc.vector.tensor_tensor(
-                out=times_sin[b][:], in0=c_f32[:, b, :, 0:ROT_ROWS], in1=sin_a, op=ALU.mult
-            )
+            times_cos[b] = rot_stage.tile([P, 2, HALF], F32, tag="times_cos", name="times_cos_%d" % b)
+            times_sin[b] = rot_stage.tile([P, 2, HALF], F32, tag="times_sin", name="times_sin_%d" % b)
+            nc.vector.tensor_tensor(out=times_cos[b][:], in0=c_rot[b][:], in1=sin_cos[:, 1], op=ALU.mult)
+            nc.vector.tensor_tensor(out=times_sin[b][:], in0=c_rot[b][:], in1=sin_cos[:, 0], op=ALU.mult)
 
         def rotate_sums(b):
             nc.vector.tensor_tensor(
-                out=c_f32[:, b, :, first_half],
-                in0=times_cos[b][:, :, first_half],
-                in1=times_sin[b][:, :, second_half],
-                op=ALU.subtract,
+                out=r_rows[:, b, 0:HALF], in0=times_cos[b][:, 0], in1=times_sin[b][:, 1], op=ALU.subtract
             )
             nc.vector.tensor_tensor(
-                out=c_f32[:, b, :, second_half],
-                in0=times_cos[b][:, :, second_half],
-                in1=times_sin[b][:, :, first_half],
-                op=ALU.add,
+                out=r_rows[:, b, HALF:DR], in0=times_cos[b][:, 1], in1=times_sin[b][:, 0], op=ALU.add
             )
 
         def transpose_r(b):
-            r_t = psum.tile([P, PACK, S], F32, tag="bank")
-            for t in range(PACK):
-                nc.tensor.transpose(out=r_t[:, t, :], in_=c_f32[:, b, t, :], identity=ident[:])
+            r_words = r_rows[:, b, :].bitcast(F32)
+            r_t = psum.tile([P, 2, S], F32, tag="bank")
+            for u in range(2):
+                nc.tensor.transpose(out=r_t[:, u, :], in_=r_words[:, u : DC // 2 : 2], identity=ident[:])
             nc.scalar.copy(
-                out=r_grouped[:, b, :].rearrange("p (r t) -> p r t", t=PACK),
-                in_=r_t[:].rearrange("p t r -> p r t"),
+                out=r_grouped[:, b, :].bitcast(F32).rearrange("p (r u) -> p r u", u=2),
+                in_=r_t[:].rearrange("p u r -> p r u"),
             )
 
         def quantise_r(b):
@@ -395,11 +381,11 @@ def tile_deepseekmla_pa_kernel(tc, x, W_c, b_c, W_d, b_d, out):
         regroup_wc(3)
         transpose_x(2)
         keep_clock_up(1)
-        transpose_x(3)
         quantise_wd(0)
         quantise_wc(3)
         quantise_x(1)
         compress(0, range(D_PASSES - 1, D_PASSES))
+        transpose_x(3)
 
         regroup_chunk(1)
         compress(1)
@@ -413,12 +399,12 @@ def tile_deepseekmla_pa_kernel(tc, x, W_c, b_c, W_d, b_d, out):
         transpose_r(0)
         regroup_wd(2, 0)
         rotate_products(1)
-        quantise_wd(1)
+        add_bc(2)
         rotate_sums(1)
         compress(3)
         transpose_r(1)
         regroup_wd(2, 1)
-        add_bc(2)
+        quantise_wd(1)
         quantise_r(0)
         multiply_pair(0, 0)
         rotate_products(2)

@@ -52,7 +52,7 @@ def tile_deepseekmla_pa_kernel(tc, x, W_c, b_c, W_d, b_d, out):
         tc.tile_pool(name="keep", bufs=1) as keep,
         tc.tile_pool(name="x_stage", bufs=B) as x_stage,
         tc.tile_pool(name="w_stage", bufs=4) as w_stage,
-        tc.tile_pool(name="rot_stage", bufs=2) as rot_stage,
+        tc.tile_pool(name="rot_stage", bufs=B) as rot_stage,
         tc.tile_pool(name="out_stage", bufs=OUT_BUFS) as out_stage,
         tc.psum_pool(name="psum", bufs=PSUM_BANKS) as psum,
         tc.manual_schedule(),
@@ -196,8 +196,6 @@ def tile_deepseekmla_pa_kernel(tc, x, W_c, b_c, W_d, b_d, out):
         x_grouped = {}
         c_ps = {}
         c_rot = {}
-        times_cos = {}
-        times_sin = {}
 
         def keep_clock_up(count):
             for i in range(count):
@@ -262,18 +260,16 @@ def tile_deepseekmla_pa_kernel(tc, x, W_c, b_c, W_d, b_d, out):
                 out=r_rows[:, b, DR:DC], in0=c_ps[b][:, DR:DC], in1=bc_all[:, DR:DC], op=ALU.add
             )
 
-        def rotate_products(b):
-            times_cos[b] = rot_stage.tile([P, 2, HALF], F32, tag="times_cos", name="times_cos_%d" % b)
-            times_sin[b] = rot_stage.tile([P, 2, HALF], F32, tag="times_sin", name="times_sin_%d" % b)
-            nc.vector.tensor_tensor(out=times_cos[b][:], in0=c_rot[b][:], in1=sin_cos[:, 1], op=ALU.mult)
-            nc.vector.tensor_tensor(out=times_sin[b][:], in0=c_rot[b][:], in1=sin_cos[:, 0], op=ALU.mult)
-
-        def rotate_sums(b):
-            nc.vector.tensor_tensor(
-                out=r_rows[:, b, 0:HALF], in0=times_cos[b][:, 0], in1=times_sin[b][:, 1], op=ALU.subtract
+        def rotate(b):
+            times_cos = rot_stage.tile([P, 2, HALF], F32, tag="times_cos", name="times_cos_%d" % b)
+            times_sin = rot_stage.tile([P, 2, HALF], F32, tag="times_sin", name="times_sin_%d" % b)
+            nc.gpsimd.tensor_tensor(out=times_cos[:], in0=c_rot[b][:], in1=sin_cos[:, 1], op=ALU.mult)
+            nc.gpsimd.tensor_tensor(out=times_sin[:], in0=c_rot[b][:], in1=sin_cos[:, 0], op=ALU.mult)
+            nc.gpsimd.tensor_tensor(
+                out=r_rows[:, b, 0:HALF], in0=times_cos[:, 0], in1=times_sin[:, 1], op=ALU.subtract
             )
-            nc.vector.tensor_tensor(
-                out=r_rows[:, b, HALF:DR], in0=times_cos[b][:, 1], in1=times_sin[b][:, 0], op=ALU.add
+            nc.gpsimd.tensor_tensor(
+                out=r_rows[:, b, HALF:DR], in0=times_cos[:, 1], in1=times_sin[:, 0], op=ALU.add
             )
 
         def transpose_r(b):
@@ -377,10 +373,9 @@ def tile_deepseekmla_pa_kernel(tc, x, W_c, b_c, W_d, b_d, out):
         compress(0, range(D_PASSES - 1))
         regroup_chunk(0)
         transpose_x(1)
-        keep_clock_up(1)
+        keep_clock_up(2)
         regroup_wc(3)
         transpose_x(2)
-        keep_clock_up(1)
         quantise_wd(0)
         quantise_wc(3)
         quantise_x(1)
@@ -389,34 +384,30 @@ def tile_deepseekmla_pa_kernel(tc, x, W_c, b_c, W_d, b_d, out):
 
         regroup_chunk(1)
         compress(1)
-        quantise_x(2)
         add_bc(0)
+        rotate(0)
+        quantise_x(2)
         quantise_x(3)
-        rotate_products(0)
         add_bc(1)
-        rotate_sums(0)
+        rotate(1)
         compress(2)
         transpose_r(0)
         regroup_wd(2, 0)
-        rotate_products(1)
         add_bc(2)
-        rotate_sums(1)
+        rotate(2)
         compress(3)
         transpose_r(1)
         regroup_wd(2, 1)
         quantise_wd(1)
         quantise_r(0)
         multiply_pair(0, 0)
-        rotate_products(2)
         add_bc(3)
-        rotate_sums(2)
+        rotate(3)
         transpose_r(2)
         finish(0, 0)
         quantise_r(1)
         multiply_pair(0, 1)
-        rotate_products(3)
         finish(1, 0)
-        rotate_sums(3)
         transpose_r(3)
         regroup_wd(3, 0)
         finish(0, 1)

import math

import concourse.mybir as mybir
from concourse.masks import make_identity

F32 = mybir.dt.float32
BF16 = mybir.dt.bfloat16
I32 = mybir.dt.int32
U32 = mybir.dt.uint32
U8 = mybir.dt.uint8
FP8X4 = mybir.dt.float8_e4m3fn_x4
ALU = mybir.AluOpType
ACT = mybir.ActivationFunctionType

P = 128
PACK = 4
K_PASS = P * PACK
N_TILE = 512

B, S, D, DC, DR = 4, 128, 2048, 512, 64
D_OUT = 3 * D
HALF = DR // 2
ROPE_BASE = 10000.0
D_PASSES = D // K_PASS

W_D_LOADS = [N_TILE] * 2 + [2 * N_TILE] * ((D_OUT // N_TILE - 2) // 2)
REGROUP_COLS = 256
CHUNKS = D_OUT // N_TILE
PSUM_BANKS = 8
OUT_BUFS = 9
PIECES = N_TILE // REGROUP_COLS
BIAS_PARTS = 2
BIAS_RUN = D_OUT // BIAS_PARTS // P
BIAS_WORDS = BIAS_RUN // 2
BIAS_WORDS_PER_BANK = N_TILE // P
ROUND_MAGIC = 1.5 * 2.0**23

FLOPS = 2 * B * S * D * DC + 2 * B * S * DC * D_OUT


def regroup_rows(copy, grouped, rows):
    copy(
        out=grouped.rearrange("p (c i) j -> p c j i", i=4),
        in_=rows.rearrange("p j (c i) -> p c j i", i=4),
    )


def tile_deepseekmla_pa_kernel(tc, x, W_c, b_c, W_d, b_d, out):
    nc = tc.nc
    with (
        tc.tile_pool(name="consts", bufs=1) as consts,
        tc.tile_pool(name="keep", bufs=1) as keep,
        tc.tile_pool(name="x_stage", bufs=B) as x_stage,
        tc.tile_pool(name="w_stage", bufs=4) as w_stage,
        tc.tile_pool(name="rot_stage", bufs=B) as rot_stage,
        tc.tile_pool(name="out_stage", bufs=OUT_BUFS) as out_stage,
        tc.psum_pool(name="psum", bufs=PSUM_BANKS) as psum,
        tc.manual_schedule(),
    ):
        wc_raw = keep.tile([P, D_PASSES, 2, 2, DC], BF16)
        wc_rows = W_c.rearrange("(g u p e) c -> g p u e c", u=2, p=P, e=2)
        x_sb = keep.tile([P, B, D], BF16)
        wd_rows = W_d.rearrange("(p j) n -> p j n", j=PACK)
        wd_raw = []

        def load_wc(g):
            nc.sync.dma_start(out=wc_raw[:, g], in_=wc_rows[g])

        def load_x(b):
            nc.sync.dma_start(out=x_sb[:, b, :], in_=x[b])

        def load_wd():
            i = len(wd_raw)
            first = sum(W_D_LOADS[:i])
            width = W_D_LOADS[i]
            raw = keep.tile([P, PACK, width], BF16, name="wd_raw_%d" % i)
            wd_raw.append((first, raw))
            nc.sync.dma_start(out=raw[:], in_=wd_rows[:, :, first : first + width])

        load_wc(0)
        bd_cols = consts.tile([P, BIAS_PARTS, BIAS_RUN], BF16)
        nc.sync.dma_start(out=bd_cols[:], in_=b_d.rearrange("(h q c) -> q h c", h=BIAS_PARTS, q=P))
        bc_cols = consts.tile([P, PACK], BF16)
        nc.sync.dma_start(out=bc_cols[:], in_=b_c.rearrange("(q c) -> q c", q=P))
        load_wc(1)
        load_x(0)
        load_wc(2)
        load_wd()
        load_wc(3)
        load_x(1)
        load_x(2)
        load_x(3)
        for i in range(1, len(W_D_LOADS)):
            load_wd()

        position = consts.tile([P, 1], F32)
        nc.gpsimd.iota(
            position[:], pattern=[[0, 1]], base=0, channel_multiplier=1,
            allow_small_or_imprecise_dtypes=True,
        )
        ident = consts.tile([P, P], F32)
        make_identity(nc, ident[:])

        sin_table_loaded = consts.tile([P, 1], F32)
        nc.scalar.activation(out=sin_table_loaded[:], in_=position[:], func=ACT.Sin, scale=0.0)
        turns = consts.tile([P, 2, HALF], F32)
        nc.vector.tensor_scalar(
            out=turns[:, 0, 0:1], in0=position[:], scalar1=1.0 / (2.0 * math.pi), scalar2=None, op0=ALU.mult
        )
        for made in (1, 2, 4, 8, 16):
            nc.vector.tensor_scalar(
                out=turns[:, 0, made : 2 * made],
                in0=turns[:, 0, 0:made],
                scalar1=ROPE_BASE ** (-2 * made / DR),
                scalar2=None,
                op0=ALU.mult,
            )
        nc.scalar.add(out=turns[:, 1], in_=turns[:, 0], add=0.25)
        whole_turns = consts.tile([P, 2, HALF], F32)
        nc.scalar.add(out=whole_turns[:], in_=turns[:], add=ROUND_MAGIC)
        minus_part_turn = consts.tile([P, 2, HALF], F32)
        sin_cos = consts.tile([P, 2, 2, HALF], F32)

        def take_off_whole_turns():
            nc.vector.scalar_tensor_tensor(
                out=minus_part_turn[:].rearrange("p s j -> p (s j)"),
                in0=whole_turns[:].rearrange("p s j -> p (s j)"),
                scalar=ROUND_MAGIC,
                in1=turns[:].rearrange("p s j -> p (s j)"),
                op0=ALU.subtract,
                op1=ALU.subtract,
            )

        def finish_sin_cos():
            for h in range(2):
                nc.scalar.activation(
                    out=sin_cos[:, :, h, :],
                    in_=minus_part_turn[:],
                    func=ACT.Sin,
                    scale=-2.0 * math.pi,
                )

        bd_all = consts.tile([P, D_OUT], BF16)
        bc_all = consts.tile([P, DC], BF16)

        def spread_bias(cols, first, count, words, dest):
            spread = psum.tile([P, count, P], F32, tag="bank")
            for u in range(count):
                w = first + u
                nc.tensor.transpose(
                    out=spread[:, u, :],
                    in_=cols.bitcast(F32)[:, w : w + 1].to_broadcast([P, P]),
                    identity=ident[:],
                )
            nc.scalar.copy(
                out=dest.bitcast(F32).rearrange("p (q u) -> p q u", u=words)[:, :, first : first + count],
                in_=spread[:].rearrange("p u q -> p q u"),
            )

        def spread_bd(part, bank):
            half = D_OUT // BIAS_PARTS
            spread_bias(
                bd_cols[:, part, :],
                bank * BIAS_WORDS_PER_BANK,
                BIAS_WORDS_PER_BANK,
                BIAS_WORDS,
                bd_all[:, part * half : (part + 1) * half],
            )

        wc_codes = keep.tile([P, D_PASSES, DC], U32, align_bytes=64)
        wc_scales = keep.tile([P, D_PASSES, DC], U8, align_bytes=64)
        wc_grouped = [
            w_stage.tile([P, DC, PACK], BF16, align_bytes=64, tag="w_grouped", name="wc_grouped_%d" % g)
            for g in range(D_PASSES)
        ]

        def quantise_wc(g):
            nc.vector.quantize_mx(
                out=wc_codes[:, g, :].bitcast(FP8X4),
                scales=wc_scales[:, g, :],
                in_=wc_grouped[g][:].rearrange("p c j -> p (c j)"),
            )

        def regroup_wc(g):
            regroup_rows(
                nc.vector.tensor_copy, wc_grouped[g][:], wc_raw[:, g].rearrange("p u e c -> p (u e) c")
            )

        x_codes = keep.tile([P, B, D_PASSES, S], U32, align_bytes=64)
        x_scales = keep.tile([P, B, D_PASSES, S], U8, align_bytes=64)
        r_rows = keep.tile([P, B, DC], BF16)
        r_grouped = keep.tile([P, B, S * PACK], BF16, align_bytes=64)
        r_codes = keep.tile([P, B, S], U32, align_bytes=64)
        r_scales = keep.tile([P, B, S], U8, align_bytes=64)

        x_grouped = {}
        c_ps = {}
        c_rot = {}

        def keep_clock_up(count):
            for i in range(count):
                unread = psum.tile([P, DC], F32, tag="bank", name="unread")
                nc.tensor.matmul(
                    out=unread[:], lhsT=wc_raw[:, 0, 0, 0, 0:P], rhs=wc_raw[:, 0, 0, 0, :], start=True, stop=True
                )

        def transpose_x(b):
            x_words = x_sb[:, b, :].bitcast(F32)
            x_grouped[b] = x_stage.tile(
                [P, D_PASSES * S * PACK], BF16, align_bytes=64, tag="x_grouped", name="x_grouped_%d" % b
            )
            x_grouped_words = x_grouped[b][:].bitcast(F32).rearrange(
                "p (g r u) -> p g r u", g=D_PASSES, u=2
            )
            for g_pair in range(0, D_PASSES, 2):
                x_t = psum.tile([P, 2, 2, S], F32, tag="bank")
                for g in range(2):
                    for u in range(2):
                        first_word = (g_pair + g) * (K_PASS // 2) + u * P
                        nc.tensor.transpose(
                            out=x_t[:, g, u, :],
                            in_=x_words[:, first_word : first_word + P],
                            identity=ident[:],
                        )
                nc.scalar.copy(
                    out=x_grouped_words[:, g_pair : g_pair + 2],
                    in_=x_t[:].rearrange("p g u r -> p g r u"),
                )

        def quantise_x(b):
            nc.vector.quantize_mx(
                out=x_codes[:, b].rearrange("p g r -> p (g r)").bitcast(FP8X4),
                scales=x_scales[:, b].rearrange("p g r -> p (g r)"),
                in_=x_grouped[b][:],
            )

        def compress(b, passes=range(D_PASSES)):
            if passes[0] == 0:
                c_ps[b] = psum.tile([P, DC], F32, tag="bank", name="c_ps_%d" % b)
            for g in passes:
                nc.tensor.matmul_mx(
                    out=c_ps[b][:],
                    lhsT=x_codes[:, b, g, :].bitcast(FP8X4),
                    lhsT_scale=x_scales[:, b, g, :],
                    rhs=wc_codes[:, g, :].bitcast(FP8X4),
                    rhs_scale=wc_scales[:, g, :],
                    start=(g == 0),
                    stop=(g == D_PASSES - 1),
                )

        def add_bc(b):
            c_rot[b] = rot_stage.tile([P, 2, HALF], F32, tag="c_rot", name="c_rot_%d" % b)
            nc.vector.tensor_tensor(
                out=c_rot[b][:].rearrange("p h j -> p (h j)"),
                in0=c_ps[b][:, 0:DR],
                in1=bc_all[:, 0:DR],
                op=ALU.add,
            )
            nc.vector.tensor_tensor(
                out=r_rows[:, b, DR:DC], in0=c_ps[b][:, DR:DC], in1=bc_all[:, DR:DC], op=ALU.add
            )

        def rotate(b):
            times_cos = rot_stage.tile([P, 2, HALF], F32, tag="times_cos", name="times_cos_%d" % b)
            times_sin = rot_stage.tile([P, 2, HALF], F32, tag="times_sin", name="times_sin_%d" % b)
            nc.gpsimd.tensor_tensor(out=times_cos[:], in0=c_rot[b][:], in1=sin_cos[:, 1], op=ALU.mult)
            nc.gpsimd.tensor_tensor(out=times_sin[:], in0=c_rot[b][:], in1=sin_cos[:, 0], op=ALU.mult)
            nc.gpsimd.tensor_tensor(
                out=r_rows[:, b, 0:HALF], in0=times_cos[:, 0], in1=times_sin[:, 1], op=ALU.subtract
            )
            nc.gpsimd.tensor_tensor(
                out=r_rows[:, b, HALF:DR], in0=times_cos[:, 1], in1=times_sin[:, 0], op=ALU.add
            )

        def transpose_r(b):
            r_words = r_rows[:, b, :].bitcast(F32)
            r_t = psum.tile([P, 2, S], F32, tag="bank")
            for u in range(2):
                nc.tensor.transpose(out=r_t[:, u, :], in_=r_words[:, u : DC // 2 : 2], identity=ident[:])
            nc.scalar.copy(
                out=r_grouped[:, b, :].bitcast(F32).rearrange("p (r u) -> p r u", u=2),
                in_=r_t[:].rearrange("p u r -> p r u"),
            )

        def quantise_r(b):
            nc.vector.quantize_mx(
                out=r_codes[:, b, :].bitcast(FP8X4),
                scales=r_scales[:, b, :],
                in_=r_grouped[:, b, :],
            )

        wd_codes = keep.tile([P, D_OUT], U32, align_bytes=64)
        wd_scales = keep.tile([P, D_OUT], U8, align_bytes=64)
        wd_grouped = {}

        def regroup_wd(n, piece):
            if piece == 0:
                wd_grouped[n] = w_stage.tile(
                    [P, N_TILE, PACK], BF16, align_bytes=64, tag="w_grouped", name="wd_grouped_%d" % n
                )
            to = piece * REGROUP_COLS
            first, raw = [load for load in wd_raw if load[0] <= n * N_TILE][-1]
            place = n * N_TILE + to - first
            regroup_rows(
                nc.scalar.copy,
                wd_grouped[n][:, to : to + REGROUP_COLS, :],
                raw[:, :, place : place + REGROUP_COLS],
            )

        def quantise_wd(n):
            cols = slice(n * N_TILE, (n + 1) * N_TILE)
            nc.vector.quantize_mx(
                out=wd_codes[:, cols].bitcast(FP8X4),
                scales=wd_scales[:, cols],
                in_=wd_grouped[n][:].rearrange("p c j -> p (c j)"),
            )

        o_ps = {}
        out_sb = {}

        def multiply(n, b):
            cols = slice(n * N_TILE, (n + 1) * N_TILE)
            o_ps[n, b] = psum.tile([P, N_TILE], F32, tag="bank", name="o_ps_%d_%d" % (n, b))
            nc.tensor.matmul_mx(
                out=o_ps[n, b][:],
                lhsT=r_codes[:, b, :].bitcast(FP8X4),
                lhsT_scale=r_scales[:, b, :],
                rhs=wd_codes[:, cols].bitcast(FP8X4),
                rhs_scale=wd_scales[:, cols],
                start=True,
                stop=True,
            )

        def finish(n, b):
            cols = slice(n * N_TILE, (n + 1) * N_TILE)
            half = n % 2
            if half == 0:
                out_sb[b] = out_stage.tile([P, 2, N_TILE], F32, tag="out_sb", name="out_sb_%d_%d" % (n, b))
            nc.vector.tensor_tensor(
                out=out_sb[b][:, half, :], in0=o_ps[n, b][:], in1=bd_all[:, cols], op=ALU.add
            )
            if n >= CHUNKS - 2:
                nc.sync.dma_start(out=out[b, :, cols], in_=out_sb[b][:, half, :])
            elif half == 1:
                nc.sync.dma_start(
                    out=out[b, :, (n - 1) * N_TILE : (n + 1) * N_TILE],
                    in_=out_sb[b][:].rearrange("p h c -> p (h c)"),
                )

        def multiply_pair(n, b):
            multiply(n, b)
            multiply(n + 1, b)

        def regroup_chunk(n):
            for piece in range(PIECES):
                regroup_wd(n, piece)

        spread_bias(bc_cols[:], 0, PACK // 2, PACK // 2, bc_all[:])
        for bank in range(BIAS_WORDS // BIAS_WORDS_PER_BANK):
            spread_bd(0, bank)

        transpose_x(0)
        keep_clock_up(4)
        regroup_wc(0)
        take_off_whole_turns()
        finish_sin_cos()
        regroup_wc(1)
        quantise_wc(0)
        quantise_wc(1)
        regroup_wc(2)
        quantise_x(0)
        quantise_wc(2)
        compress(0, range(D_PASSES - 1))
        regroup_chunk(0)
        transpose_x(1)
        keep_clock_up(2)
        regroup_wc(3)
        transpose_x(2)
        quantise_wd(0)
        quantise_wc(3)
        quantise_x(1)
        compress(0, range(D_PASSES - 1, D_PASSES))
        transpose_x(3)

        regroup_chunk(1)
        compress(1)
        add_bc(0)
        rotate(0)
        quantise_x(2)
        quantise_x(3)
        add_bc(1)
        rotate(1)
        compress(2)
        transpose_r(0)
        regroup_wd(2, 0)
        add_bc(2)
        rotate(2)
        compress(3)
        transpose_r(1)
        regroup_wd(2, 1)
        quantise_wd(1)
        quantise_r(0)
        multiply_pair(0, 0)
        add_bc(3)
        rotate(3)
        transpose_r(2)
        finish(0, 0)
        quantise_r(1)
        multiply_pair(0, 1)
        finish(1, 0)
        transpose_r(3)
        regroup_wd(3, 0)
        finish(0, 1)
        quantise_r(2)
        multiply_pair(0, 2)
        regroup_wd(3, 1)
        finish(1, 1)
        quantise_wd(2)
        finish(0, 2)
        quantise_r(3)
        multiply_pair(0, 3)
        finish(1, 2)
        finish(0, 3)
        quantise_wd(3)
        finish(1, 3)

        for n in range(2, CHUNKS - 2, 2):
            for m in (n + 2, n + 3):
                regroup_chunk(m)
                bank = m - 5
                if bank in range(BIAS_WORDS // BIAS_WORDS_PER_BANK):
                    spread_bd(1, bank)
            for b in range(B):
                multiply_pair(n, b)
            for b in range(B):
                if b >= B - 2 and n + b < CHUNKS - 1:
                    quantise_wd(n + b)
                finish(n, b)
                finish(n + 1, b)

        for n in range(CHUNKS - 2, CHUNKS):
            for b in range(B):
                multiply(n, b)
            for b in range(B):
                if b == B // 2 and n + 1 < CHUNKS:
                    quantise_wd(n + 1)
                finish(n, b)
